import numpy as np
import ml_dtypes


def mxq(x, axis, fmt="e4m3"):
    dtype, down = {"e4m3": (ml_dtypes.float8_e4m3fn, 7), "e5m2": (ml_dtypes.float8_e5m2, 14)}[fmt]
    v = np.moveaxis(np.asarray(x, np.float32).astype(ml_dtypes.bfloat16).astype(np.float64), axis, -1)
    blocks = v.reshape(v.shape[:-1] + (-1, 32))
    amax = np.abs(blocks).max(-1, keepdims=True)
    byte = np.maximum(np.where(amax > 0, np.frexp(amax)[1] - 1 + 127, 0) - down, 1)
    scale = np.exp2(byte - 127.0)
    codes = (blocks / scale).astype(np.float32).astype(dtype).astype(np.float64)
    return np.moveaxis((codes * scale).reshape(v.shape), -1, axis)


WIDE = False


def mx_kscale(k):
    if not WIDE:
        return np.ones(k)
    levels = np.array([10, -10, 5, -5, 0])
    a = np.random.permutation(np.resize(levels, k // 512 * 4)).reshape(k // 512, 4)
    idx = np.arange(k)
    return np.exp2(a[idx // 512, idx % 128 // 32])


BF16 = ml_dtypes.bfloat16


def bf(x):
    return np.asarray(x, np.float32).astype(BF16)


def f64(x):
    return np.asarray(x).astype(np.float64)


E2M1 = np.array([0.0, 0.5, 1.0, 1.5, 2.0, 3.0, 4.0, 6.0, -0.0, -0.5, -1.0, -1.5, -2.0, -3.0, -4.0, -6.0])


def pack_weight(w, fmt):
    k, n = w.shape
    w = f64(bf(w)).reshape(k // 32, 32, n)
    amax = np.abs(w).max(1)
    if fmt == "e4m3":
        byte = np.frexp(amax)[1] - 1 + 127 - 7
    else:
        mant, ex = np.frexp(amax / 6.0)
        byte = np.where(mant > 0.5, ex, ex - 1) + 127
    byte = np.clip(np.where(amax > 0, byte, 1), 1, 254)
    scaled = (w * np.exp2(127.0 - byte)[:, None, :]).reshape(k, n).astype(np.float32)
    by_word = np.ascontiguousarray(scaled.reshape(k // 512, 128, 4, n).transpose(0, 1, 3, 2))
    if fmt == "e4m3":
        words = by_word.astype(ml_dtypes.float8_e4m3fn).view(np.uint8)
    else:
        c = by_word.astype(ml_dtypes.float4_e2m1fn).view(np.uint8) & 0xF
        words = c[..., 0::2] | (c[..., 1::2] << 4)
    return np.ascontiguousarray(words), np.ascontiguousarray(byte.astype(np.uint8).reshape(k // 512, 16, n))


def unpack_weight(words, scales, fmt):
    g, p, n, _ = words.shape
    if fmt == "e4m3":
        vals = np.ascontiguousarray(words).view(ml_dtypes.float8_e4m3fn).astype(np.float64)
    else:
        nib = np.empty((g, p, n, 4), np.uint8)
        nib[..., 0::2] = words & 0xF
        nib[..., 1::2] = words >> 4
        vals = E2M1[nib]
    vals = vals * np.repeat(np.exp2(scales.astype(np.float64) - 127.0), 8, axis=1)[..., None]
    return vals.transpose(0, 1, 3, 2).reshape(g * 512, n)


B, N, H, R, L = 8, 512, 512, 2, 2
NEG_INF = -1e30


def setup_inputs():
    s = mx_kscale(H)
    adj = bf(np.random.uniform(size=(B, N, N, R)) * 4.0)
    x = bf(np.random.standard_normal((B, N, H)) * s)
    dmask = bf(np.random.uniform(size=(B, 1, N)) > 0.1)
    stack = np.random.standard_normal((R, H, H)) * 1.5 / np.sqrt(H) / s[:, None]
    words, scales = pack_weight(stack.reshape(-1, H), "e4m3")
    return {"adj": adj,
            "x": x,
            "dmask": dmask,
            "W_words": words,
            "W_scales": scales}


def reference(adj, x, dmask, W_words, W_scales):
    a = f64(adj).transpose(0, 3, 1, 2)
    m = f64(dmask)[:, None, :, :]
    logits = a * m + (1.0 - m) * NEG_INF
    e = np.exp(logits - logits.max(-1, keepdims=True))
    att = e / e.sum(-1, keepdims=True)
    h = mxq(f64(x), 2, "e4m3")[:, None] @ unpack_weight(W_words, W_scales, "e4m3").reshape(R, H, H)[None]
    g = np.maximum(mxq(att, 3, "e4m3") @ mxq(h, 2, "e4m3"), 0.0)
    return g.sum(1)

@@ -1,0 +1,229 @@
+from contextlib import ExitStack
+
+import concourse.bass as bass
+import concourse.mybir as mybir
+import concourse.tile as tile
+from concourse.masks import make_identity
+
+F32 = mybir.dt.float32
+BF16 = mybir.dt.bfloat16
+I32 = mybir.dt.int32
+U32 = mybir.dt.uint32
+U8 = mybir.dt.uint8
+FP8X4 = mybir.dt.float8_e4m3fn_x4
+ALU = mybir.AluOpType
+FUNC = mybir.ActivationFunctionType
+AXIS = mybir.AxisListType
+
+GRAPHS = 8
+NODES = 512
+FEATS = 512
+RELS = 2
+P = 128
+PACK = 4
+TILES = NODES // P
+BIG = 1.0e30
+
+FLOPS = 2 * GRAPHS * RELS * NODES * FEATS * FEATS + 2 * GRAPHS * RELS * NODES * NODES * FEATS
+
+
+def tile_rgat_pa_t_e_kernel(tc, adj, x, dmask, W_words, W_scales, out):
+    nc = tc.nc
+    with ExitStack() as stack:
+        consts = stack.enter_context(tc.tile_pool(name="consts", bufs=1))
+        loads = stack.enter_context(tc.tile_pool(name="loads", bufs=3))
+        work = stack.enter_context(tc.tile_pool(name="work", bufs=2))
+        stats = stack.enter_context(tc.tile_pool(name="stats", bufs=3))
+        psum_x = stack.enter_context(tc.psum_pool(name="psum_x", bufs=1))
+        psum_h = stack.enter_context(tc.psum_pool(name="psum_h", bufs=2))
+        psum_a = stack.enter_context(tc.psum_pool(name="psum_a", bufs=2))
+        psum_g = stack.enter_context(tc.psum_pool(name="psum_g", bufs=3))
+
+        ident = consts.tile([P, P], F32)
+        make_identity(nc, ident[:])
+        w_codes = consts.tile([P, RELS, FEATS], U32, align_bytes=64)
+        w_scales = consts.tile([P, RELS, FEATS], U8, align_bytes=64)
+        nc.vector.memset(w_scales[:].bitcast(I32), 0)
+
+        def load(b):
+            mask_b = loads.tile([P, NODES], BF16, name="mask_b")
+            nc.sync.dma_start(out=mask_b[:], in_=dmask[b, 0, :].partition_broadcast(P))
+            adj_sb = loads.tile([P, TILES, NODES * RELS], BF16, name="adj_sb")
+            nc.sync.dma_start(out=adj_sb[:], in_=adj[b].rearrange("(p j) m r -> p j (m r)", j=TILES))
+            x_sb = loads.tile([P, PACK, FEATS], BF16, name="x_sb")
+            nc.sync.dma_start(
+                out=x_sb[:].rearrange("p (u e) k -> p u e k", u=2),
+                in_=x[b].rearrange("(u p e) k -> p u e k", u=2, e=2),
+            )
+            return mask_b, adj_sb, x_sb
+
+        loaded = {0: load(0)}
+        for quad in range(4):
+            nc.sync.dma_start(
+                out=w_scales[32 * quad : 32 * quad + 4, :, :].bitcast(I32),
+                in_=W_scales[:, 4 * quad : 4 * quad + 4, :].rearrange("g q n -> q g n").bitcast(I32),
+            )
+        nc.sync.dma_start(
+            out=w_codes[:].bitcast(I32),
+            in_=W_words.rearrange("g p n t -> p g (n t)").bitcast(I32),
+        )
+        loaded[1] = load(1)
+
+        for b in range(GRAPHS):
+            if b + 2 < GRAPHS:
+                loaded[b + 2] = load(b + 2)
+            mask_b, adj_sb, x_sb = loaded[b]
+
+            xg = work.tile([P, PACK, P, PACK], BF16, name="xg", align_bytes=64)
+            for half in range(2):
+                xT = psum_x.tile([P, 2, 2, P], F32, name="xT")
+                for tt in range(2):
+                    words = x_sb[:, 2 * half + tt, :].bitcast(F32)
+                    for v in range(2):
+                        nc.tensor.transpose(xT[:, tt, v, :], words[:, v : FEATS // 2 : 2], ident[:])
+                nc.scalar.copy(
+                    out=xg[:, 2 * half : 2 * half + 2, :, :].bitcast(F32),
+                    in_=xT[:].rearrange("p tt v n -> p tt n v"),
+                )
+            x_codes = work.tile([P, NODES], U32, name="x_codes", align_bytes=64)
+            x_scales = work.tile([P, NODES], U8, name="x_scales", align_bytes=64)
+            nc.vector.quantize_mx(
+                out=x_codes[:].bitcast(FP8X4),
+                scales=x_scales[:],
+                in_=xg[:].rearrange("p t n k -> p (t n k)"),
+            )
+            hg = work.tile([P, RELS, FEATS, PACK], BF16, name="hg", align_bytes=64)
+            h_codes = work.tile([P, RELS, FEATS], U32, name="h_codes", align_bytes=64)
+            h_scales = work.tile([P, RELS, FEATS], U8, name="h_scales", align_bytes=64)
+            for r in range(RELS):
+                for c in range(FEATS // P):
+                    cols = slice(c * P, (c + 1) * P)
+                    hps = psum_h.tile([P, PACK, P], F32, name="hps")
+                    for t in range(PACK):
+                        rows = slice(t * P, (t + 1) * P)
+                        nc.tensor.matmul_mx(
+                            out=hps[:, t, :],
+                            lhsT=x_codes[:, rows].bitcast(FP8X4),
+                            lhsT_scale=x_scales[:, rows],
+                            rhs=w_codes[:, r, cols].bitcast(FP8X4),
+                            rhs_scale=w_scales[:, r, cols],
+                            start=True,
+                            stop=True,
+                        )
+                    nc.scalar.copy(out=hg[:, r, cols, :], in_=hps[:].rearrange("p t c -> p c t"))
+                nc.vector.quantize_mx(
+                    out=h_codes[:, r, :].bitcast(FP8X4),
+                    scales=h_scales[:, r, :],
+                    in_=hg[:, r, :, :].rearrange("p c t -> p (c t)"),
+                )
+
+            neg = work.tile([P, NODES, RELS], BF16, name="neg")
+            nc.gpsimd.tensor_scalar(
+                out=neg[:],
+                in0=mask_b[:].unsqueeze(2).to_broadcast([P, NODES, RELS]),
+                scalar1=BIG,
+                scalar2=-BIG,
+                op0=ALU.mult,
+                op1=ALU.add,
+            )
+            nc.vector.tensor_tensor(
+                out=adj_sb[:],
+                in0=adj_sb[:],
+                in1=neg[:].rearrange("p m r -> p (m r)").unsqueeze(1).to_broadcast([P, TILES, NODES * RELS]),
+                op=ALU.add,
+            )
+            width = NODES * RELS // 2
+            fold1 = work.tile([P, TILES, width], BF16, name="fold1")
+            nc.vector.tensor_tensor(out=fold1[:], in0=adj_sb[:, :, 0:width], in1=adj_sb[:, :, width : 2 * width], op=ALU.max)
+            width = width // 2
+            fold2 = work.tile([P, TILES, width], BF16, name="fold2")
+            nc.vector.tensor_tensor(out=fold2[:], in0=fold1[:, :, 0:width], in1=fold1[:, :, width : 2 * width], op=ALU.max)
+            width = width // 2
+            fold3 = work.tile([P, TILES, width], BF16, name="fold3")
+            nc.vector.tensor_tensor(out=fold3[:], in0=fold2[:, :, 0:width], in1=fold2[:, :, width : 2 * width], op=ALU.max)
+            negmax = stats.tile([P, TILES, RELS], F32, name="negmax")
+            nc.vector.tensor_reduce(
+                out=negmax[:],
+                in_=fold3[:].rearrange("p j (m r) -> p j r m", r=RELS),
+                axis=AXIS.X,
+                op=ALU.max,
+                negate=True,
+            )
+            e = work.tile([P, TILES, RELS, NODES], F32, name="e")
+            sums = stats.tile([P, TILES, RELS], F32, name="sums")
+            for j in range(TILES):
+                by_rel = adj_sb[:, j, :].rearrange("p (m r) -> p r m", r=RELS)
+                for r in range(RELS):
+                    nc.scalar.activation(
+                        out=e[:, j, r, :],
+                        in_=by_rel[:, r, :],
+                        func=FUNC.Exp,
+                        bias=negmax[:, j, r : r + 1],
+                        scale=1.0,
+                        accum_out=sums[:, j, r : r + 1],
+                    )
+            recip = stats.tile([P, TILES, RELS], F32, name="recip")
+            nc.vector.reciprocal(out=recip[:], in_=sums[:])
+            att = work.tile([P, TILES, RELS, NODES], BF16, name="att")
+            for j in range(TILES):
+                for r in range(RELS):
+                    nc.vector.tensor_scalar(
+                        out=att[:, j, r, :],
+                        in0=e[:, j, r, :],
+                        scalar1=recip[:, j, r : r + 1],
+                        scalar2=None,
+                        op0=ALU.mult,
+                    )
+
+            attg = work.tile([P, RELS, TILES, P, PACK], BF16, name="attg", align_bytes=64)
+            att_codes = work.tile([P, RELS, NODES], U32, name="att_codes", align_bytes=64)
+            att_scales = work.tile([P, RELS, NODES], U8, name="att_scales", align_bytes=64)
+            for r in range(RELS):
+                for half in range(2):
+                    aT = psum_a.tile([P, 2, 2, P], F32, name="aT")
+                    for jj in range(2):
+                        words = att[:, 2 * half + jj, r, :].bitcast(F32)
+                        for u in range(2):
+                            nc.tensor.transpose(aT[:, jj, u, :], words[:, u * P : (u + 1) * P], ident[:])
+                    copy_out = nc.vector.tensor_copy if half == 0 else nc.scalar.copy
+                    copy_out(
+                        out=attg[:, r, 2 * half : 2 * half + 2, :, :].bitcast(F32),
+                        in_=aT[:].rearrange("p jj u n -> p jj n u"),
+                    )
+                nc.vector.quantize_mx(
+                    out=att_codes[:, r, :].bitcast(FP8X4),
+                    scales=att_scales[:, r, :],
+                    in_=attg[:, r, :, :, :].rearrange("p j n t -> p (j n t)"),
+                )
+
+            out_sb = work.tile([P, TILES, FEATS], F32, name="out_sb")
+            for j in range(TILES):
+                rows = slice(j * P, (j + 1) * P)
+                g = []
+                for r in range(RELS):
+                    g_r = psum_g.tile([P, FEATS], F32, name="g_r")
+                    nc.tensor.matmul_mx(
+                        out=g_r[:],
+                        lhsT=att_codes[:, r, rows].bitcast(FP8X4),
+                        lhsT_scale=att_scales[:, r, rows],
+                        rhs=h_codes[:, r, :].bitcast(FP8X4),
+                        rhs_scale=h_scales[:, r, :],
+                        start=True,
+                        stop=True,
+                    )
+                    g.append(g_r)
+                relu0 = stats.tile([P, FEATS], F32, name="relu0")
+                nc.scalar.activation(out=relu0[:], in_=g[0][:], func=FUNC.Relu)
+                nc.vector.scalar_tensor_tensor(
+                    out=out_sb[:, j, :],
+                    in0=g[1][:],
+                    scalar=0.0,
+                    in1=relu0[:],
+                    op0=ALU.max,
+                    op1=ALU.add,
+                )
+                if j % 2 == 1:
+                    nc.gpsimd.dma_start(
+                        out=out[b].rearrange("(p j) h -> p j h", j=TILES)[:, j - 1 : j + 1, :],
+                        in_=out_sb[:, j - 1 : j + 1, :],
+                    )

@@ -1,8 +1,6 @@
 from contextlib import ExitStack
 
-import concourse.bass as bass
 import concourse.mybir as mybir
-import concourse.tile as tile
 from concourse.masks import make_identity
 
 F32 = mybir.dt.float32
@@ -23,6 +21,7 @@ P = 128
 PACK = 4
 TILES = NODES // P
 BIG = 1.0e30
+FOLDS = 3
 
 FLOPS = 2 * GRAPHS * RELS * NODES * FEATS * FEATS + 2 * GRAPHS * RELS * NODES * NODES * FEATS
 
@@ -31,128 +30,113 @@ def tile_rgat_pa_t_e_kernel(tc, adj, x, dmask, W_words, W_scales, out):
     nc = tc.nc
     with ExitStack() as stack:
         consts = stack.enter_context(tc.tile_pool(name="consts", bufs=1))
-        loads = stack.enter_context(tc.tile_pool(name="loads", bufs=3))
-        work = stack.enter_context(tc.tile_pool(name="work", bufs=2))
-        stats = stack.enter_context(tc.tile_pool(name="stats", bufs=3))
-        psum_x = stack.enter_context(tc.psum_pool(name="psum_x", bufs=1))
-        psum_h = stack.enter_context(tc.psum_pool(name="psum_h", bufs=2))
-        psum_a = stack.enter_context(tc.psum_pool(name="psum_a", bufs=2))
-        psum_g = stack.enter_context(tc.psum_pool(name="psum_g", bufs=3))
+        pool2 = stack.enter_context(tc.tile_pool(name="pool2", bufs=2))
+        pool3 = stack.enter_context(tc.tile_pool(name="pool3", bufs=3))
+        psum = stack.enter_context(tc.psum_pool(name="psum", bufs=8))
+
+        held = {}
+
+        def graph(b):
+            return 0 <= b < GRAPHS
 
         ident = consts.tile([P, P], F32)
         make_identity(nc, ident[:])
+        ident_bf = consts.tile([P, P], BF16)
+        make_identity(nc, ident_bf[:])
         w_codes = consts.tile([P, RELS, FEATS], U32, align_bytes=64)
         w_scales = consts.tile([P, RELS, FEATS], U8, align_bytes=64)
         nc.vector.memset(w_scales[:].bitcast(I32), 0)
+        mask_rows = consts.tile([P, NODES], BF16)
+        nc.vector.memset(mask_rows[:], 0.0)
+        nc.sync.dma_start(out=mask_rows[0:GRAPHS, :], in_=dmask.rearrange("b o m -> (b o) m"))
+        neg_rows = consts.tile([P, NODES], BF16)
+        nc.vector.tensor_scalar(out=neg_rows[:], in0=mask_rows[:], scalar1=BIG, scalar2=-BIG, op0=ALU.mult, op1=ALU.add)
 
-        def load(b):
-            mask_b = loads.tile([P, NODES], BF16, name="mask_b")
-            nc.sync.dma_start(out=mask_b[:], in_=dmask[b, 0, :].partition_broadcast(P))
-            adj_sb = loads.tile([P, TILES, NODES * RELS], BF16, name="adj_sb")
-            nc.sync.dma_start(out=adj_sb[:], in_=adj[b].rearrange("(p j) m r -> p j (m r)", j=TILES))
-            x_sb = loads.tile([P, PACK, FEATS], BF16, name="x_sb")
+        def load_x(b):
+            if not graph(b):
+                return
+            x_sb = pool2.tile([P, PACK, FEATS], BF16, name="x_sb")
             nc.sync.dma_start(
                 out=x_sb[:].rearrange("p (u e) k -> p u e k", u=2),
                 in_=x[b].rearrange("(u p e) k -> p u e k", u=2, e=2),
             )
-            return mask_b, adj_sb, x_sb
+            held["x_sb", b] = x_sb
 
-        loaded = {0: load(0)}
-        for quad in range(4):
+        def load_weight():
+            for quad in range(4):
+                nc.sync.dma_start(
+                    out=w_scales[32 * quad : 32 * quad + 4, :, :].bitcast(I32),
+                    in_=W_scales[:, 4 * quad : 4 * quad + 4, :].rearrange("g q n -> q g n").bitcast(I32),
+                )
             nc.sync.dma_start(
-                out=w_scales[32 * quad : 32 * quad + 4, :, :].bitcast(I32),
-                in_=W_scales[:, 4 * quad : 4 * quad + 4, :].rearrange("g q n -> q g n").bitcast(I32),
+                out=w_codes[:].bitcast(I32),
+                in_=W_words.rearrange("g p n t -> p g (n t)").bitcast(I32),
             )
-        nc.sync.dma_start(
-            out=w_codes[:].bitcast(I32),
-            in_=W_words.rearrange("g p n t -> p g (n t)").bitcast(I32),
-        )
-        loaded[1] = load(1)
 
-        for b in range(GRAPHS):
-            if b + 2 < GRAPHS:
-                loaded[b + 2] = load(b + 2)
-            mask_b, adj_sb, x_sb = loaded[b]
+        def load_adj(b):
+            if not graph(b):
+                return
+            adj_sb = pool3.tile([P, TILES, NODES * RELS], BF16, name="adj_sb")
+            nc.sync.dma_start(out=adj_sb[:], in_=adj[b].rearrange("(p j) m r -> p j (m r)", j=TILES))
+            held["level", 0, b] = adj_sb
 
-            xg = work.tile([P, PACK, P, PACK], BF16, name="xg", align_bytes=64)
+        def spread_mask(b):
+            if not graph(b):
+                return
+            neg = psum.tile([P, NODES, RELS], BF16, name="neg", tag="bank")
             for half in range(2):
-                xT = psum_x.tile([P, 2, 2, P], F32, name="xT")
-                for tt in range(2):
-                    words = x_sb[:, 2 * half + tt, :].bitcast(F32)
-                    for v in range(2):
-                        nc.tensor.transpose(xT[:, tt, v, :], words[:, v : FEATS // 2 : 2], ident[:])
-                nc.scalar.copy(
-                    out=xg[:, 2 * half : 2 * half + 2, :, :].bitcast(F32),
-                    in_=xT[:].rearrange("p tt v n -> p tt n v"),
+                keys = slice(half * NODES // 2, (half + 1) * NODES // 2)
+                nc.tensor.matmul(
+                    out=neg[:, keys, :],
+                    lhsT=ident_bf[:, b : b + 1].to_broadcast([P, P]),
+                    rhs=neg_rows[:, keys].unsqueeze(2).to_broadcast([P, NODES // 2, RELS]),
+                    start=True,
+                    stop=True,
                 )
-            x_codes = work.tile([P, NODES], U32, name="x_codes", align_bytes=64)
-            x_scales = work.tile([P, NODES], U8, name="x_scales", align_bytes=64)
-            nc.vector.quantize_mx(
-                out=x_codes[:].bitcast(FP8X4),
-                scales=x_scales[:],
-                in_=xg[:].rearrange("p t n k -> p (t n k)"),
-            )
-            hg = work.tile([P, RELS, FEATS, PACK], BF16, name="hg", align_bytes=64)
-            h_codes = work.tile([P, RELS, FEATS], U32, name="h_codes", align_bytes=64)
-            h_scales = work.tile([P, RELS, FEATS], U8, name="h_scales", align_bytes=64)
-            for r in range(RELS):
-                for c in range(FEATS // P):
-                    cols = slice(c * P, (c + 1) * P)
-                    hps = psum_h.tile([P, PACK, P], F32, name="hps")
-                    for t in range(PACK):
-                        rows = slice(t * P, (t + 1) * P)
-                        nc.tensor.matmul_mx(
-                            out=hps[:, t, :],
-                            lhsT=x_codes[:, rows].bitcast(FP8X4),
-                            lhsT_scale=x_scales[:, rows],
-                            rhs=w_codes[:, r, cols].bitcast(FP8X4),
-                            rhs_scale=w_scales[:, r, cols],
-                            start=True,
-                            stop=True,
-                        )
-                    nc.scalar.copy(out=hg[:, r, cols, :], in_=hps[:].rearrange("p t c -> p c t"))
-                nc.vector.quantize_mx(
-                    out=h_codes[:, r, :].bitcast(FP8X4),
-                    scales=h_scales[:, r, :],
-                    in_=hg[:, r, :, :].rearrange("p c t -> p (c t)"),
-                )
+            held["neg", b] = neg
 
-            neg = work.tile([P, NODES, RELS], BF16, name="neg")
-            nc.gpsimd.tensor_scalar(
-                out=neg[:],
-                in0=mask_b[:].unsqueeze(2).to_broadcast([P, NODES, RELS]),
-                scalar1=BIG,
-                scalar2=-BIG,
-                op0=ALU.mult,
-                op1=ALU.add,
-            )
+        def add_mask(b):
+            if not graph(b):
+                return
+            adj_sb = held["level", 0, b]
             nc.vector.tensor_tensor(
                 out=adj_sb[:],
                 in0=adj_sb[:],
-                in1=neg[:].rearrange("p m r -> p (m r)").unsqueeze(1).to_broadcast([P, TILES, NODES * RELS]),
+                in1=held["neg", b][:].rearrange("p m r -> p (m r)").unsqueeze(1).to_broadcast([P, TILES, NODES * RELS]),
                 op=ALU.add,
             )
-            width = NODES * RELS // 2
-            fold1 = work.tile([P, TILES, width], BF16, name="fold1")
-            nc.vector.tensor_tensor(out=fold1[:], in0=adj_sb[:, :, 0:width], in1=adj_sb[:, :, width : 2 * width], op=ALU.max)
-            width = width // 2
-            fold2 = work.tile([P, TILES, width], BF16, name="fold2")
-            nc.vector.tensor_tensor(out=fold2[:], in0=fold1[:, :, 0:width], in1=fold1[:, :, width : 2 * width], op=ALU.max)
-            width = width // 2
-            fold3 = work.tile([P, TILES, width], BF16, name="fold3")
-            nc.vector.tensor_tensor(out=fold3[:], in0=fold2[:, :, 0:width], in1=fold2[:, :, width : 2 * width], op=ALU.max)
-            negmax = stats.tile([P, TILES, RELS], F32, name="negmax")
+
+        def fold(b, level):
+            if not graph(b):
+                return
+            width = (NODES * RELS) >> level
+            before = held["level", level - 1, b]
+            after = pool2.tile([P, TILES, width], BF16, name="fold%d" % level)
+            nc.vector.tensor_tensor(out=after[:], in0=before[:, :, 0:width], in1=before[:, :, width : 2 * width], op=ALU.max)
+            held["level", level, b] = after
+
+        def reduce_max(b):
+            if not graph(b):
+                return
+            negmax = pool3.tile([P, TILES, RELS], F32, name="negmax")
             nc.vector.tensor_reduce(
                 out=negmax[:],
-                in_=fold3[:].rearrange("p j (m r) -> p j r m", r=RELS),
+                in_=held["level", FOLDS, b][:].rearrange("p j (m r) -> p j r m", r=RELS),
                 axis=AXIS.X,
                 op=ALU.max,
                 negate=True,
             )
-            e = work.tile([P, TILES, RELS, NODES], F32, name="e")
-            sums = stats.tile([P, TILES, RELS], F32, name="sums")
+            held["negmax", b] = negmax
+
+        def exponentials(b):
+            if not graph(b):
+                return
+            logits = held["level", 0, b]
+            negmax = held["negmax", b]
+            e = pool2.tile([P, TILES, RELS, NODES], F32, name="e")
+            sums = pool3.tile([P, TILES, RELS], F32, name="sums")
             for j in range(TILES):
-                by_rel = adj_sb[:, j, :].rearrange("p (m r) -> p r m", r=RELS)
+                by_rel = logits[:, j, :].rearrange("p (m r) -> p r m", r=RELS)
                 for r in range(RELS):
                     nc.scalar.activation(
                         out=e[:, j, r, :],
@@ -162,9 +146,16 @@ def tile_rgat_pa_t_e_kernel(tc, adj, x, dmask, W_words, W_scales, out):
                         scale=1.0,
                         accum_out=sums[:, j, r : r + 1],
                     )
-            recip = stats.tile([P, TILES, RELS], F32, name="recip")
-            nc.vector.reciprocal(out=recip[:], in_=sums[:])
-            att = work.tile([P, TILES, RELS, NODES], BF16, name="att")
+            held["e", b] = e
+            held["sums", b] = sums
+
+        def normalise(b):
+            if not graph(b):
+                return
+            e = held["e", b]
+            recip = pool2.tile([P, TILES, RELS], F32, name="recip")
+            nc.vector.reciprocal(out=recip[:], in_=held["sums", b][:])
+            att = pool2.tile([P, TILES, RELS, NODES], BF16, name="att")
             for j in range(TILES):
                 for r in range(RELS):
                     nc.vector.tensor_scalar(
@@ -174,45 +165,125 @@ def tile_rgat_pa_t_e_kernel(tc, adj, x, dmask, W_words, W_scales, out):
                         scalar2=None,
                         op0=ALU.mult,
                     )
+            held["att", b] = att
 
-            attg = work.tile([P, RELS, TILES, P, PACK], BF16, name="attg", align_bytes=64)
-            att_codes = work.tile([P, RELS, NODES], U32, name="att_codes", align_bytes=64)
-            att_scales = work.tile([P, RELS, NODES], U8, name="att_scales", align_bytes=64)
-            for r in range(RELS):
-                for half in range(2):
-                    aT = psum_a.tile([P, 2, 2, P], F32, name="aT")
+        def transpose_att(b):
+            if not graph(b):
+                return
+            att = held["att", b]
+            held["attg", b] = pool2.tile([P, RELS, TILES, P, PACK], BF16, name="attg", align_bytes=64)
+            for half in range(2):
+                for r in range(RELS):
+                    aT = psum.tile([P, 2, 2, P], F32, name="aT", tag="bank")
                     for jj in range(2):
                         words = att[:, 2 * half + jj, r, :].bitcast(F32)
                         for u in range(2):
                             nc.tensor.transpose(aT[:, jj, u, :], words[:, u * P : (u + 1) * P], ident[:])
-                    copy_out = nc.vector.tensor_copy if half == 0 else nc.scalar.copy
-                    copy_out(
-                        out=attg[:, r, 2 * half : 2 * half + 2, :, :].bitcast(F32),
-                        in_=aT[:].rearrange("p jj u n -> p jj n u"),
-                    )
-                nc.vector.quantize_mx(
-                    out=att_codes[:, r, :].bitcast(FP8X4),
-                    scales=att_scales[:, r, :],
-                    in_=attg[:, r, :, :, :].rearrange("p j n t -> p (j n t)"),
-                )
+                    held["aT", half, r, b] = aT
 
-            out_sb = work.tile([P, TILES, FEATS], F32, name="out_sb")
+        def copy_att(b, half, r, copy_out):
+            if not graph(b):
+                return
+            copy_out(
+                out=held["attg", b][:, r, 2 * half : 2 * half + 2, :, :].bitcast(F32),
+                in_=held["aT", half, r, b][:].rearrange("p jj u n -> p jj n u"),
+            )
+
+        def quantise_att(b, r):
+            if not graph(b):
+                return
+            if r == 0:
+                held["att_codes", b] = pool2.tile([P, RELS, NODES], U32, name="att_codes", align_bytes=64)
+                held["att_scales", b] = pool2.tile([P, RELS, NODES], U8, name="att_scales", align_bytes=64)
+            nc.vector.quantize_mx(
+                out=held["att_codes", b][:, r, :].bitcast(FP8X4),
+                scales=held["att_scales", b][:, r, :],
+                in_=held["attg", b][:, r, :, :, :].rearrange("p j n t -> p (j n t)"),
+            )
+
+        def transpose_x(b, half):
+            if not graph(b):
+                return
+            x_sb = held["x_sb", b]
+            if half == 0:
+                held["xg", b] = pool2.tile([P, PACK, P, PACK], BF16, name="xg", align_bytes=64)
+            xg = held["xg", b]
+            xT = psum.tile([P, 2, 2, P], F32, name="xT", tag="bank")
+            for tt in range(2):
+                words = x_sb[:, 2 * half + tt, :].bitcast(F32)
+                for v in range(2):
+                    nc.tensor.transpose(xT[:, tt, v, :], words[:, v : FEATS // 2 : 2], ident[:])
+            nc.scalar.copy(
+                out=xg[:, 2 * half : 2 * half + 2, :, :].bitcast(F32),
+                in_=xT[:].rearrange("p tt v n -> p tt n v"),
+            )
+            if half == 1:
+                x_codes = pool2.tile([P, NODES], U32, name="x_codes", align_bytes=64)
+                x_scales = pool2.tile([P, NODES], U8, name="x_scales", align_bytes=64)
+                nc.vector.quantize_mx(
+                    out=x_codes[:].bitcast(FP8X4),
+                    scales=x_scales[:],
+                    in_=xg[:].rearrange("p t n k -> p (t n k)"),
+                )
+                held["x_codes", b] = x_codes
+                held["x_scales", b] = x_scales
+
+        def project(b, r):
+            if not graph(b):
+                return
+            x_codes = held["x_codes", b]
+            x_scales = held["x_scales", b]
+            hg = pool2.tile([P, FEATS, PACK], BF16, name="hg", align_bytes=64)
+            for c in range(FEATS // P):
+                cols = slice(c * P, (c + 1) * P)
+                hps = psum.tile([P, PACK, P], F32, name="hps", tag="bank")
+                for t in range(PACK):
+                    rows = slice(t * P, (t + 1) * P)
+                    nc.tensor.matmul_mx(
+                        out=hps[:, t, :],
+                        lhsT=x_codes[:, rows].bitcast(FP8X4),
+                        lhsT_scale=x_scales[:, rows],
+                        rhs=w_codes[:, r, cols].bitcast(FP8X4),
+                        rhs_scale=w_scales[:, r, cols],
+                        start=True,
+                        stop=True,
+                    )
+                nc.scalar.copy(out=hg[:, cols, :], in_=hps[:].rearrange("p t c -> p c t"))
+            held["hg", r, b] = hg
+
+        def quantise_h(b, r):
+            if not graph(b):
+                return
+            if r == 0:
+                held["h_codes", b] = pool3.tile([P, RELS, FEATS], U32, name="h_codes", align_bytes=64)
+                held["h_scales", b] = pool3.tile([P, RELS, FEATS], U8, name="h_scales", align_bytes=64)
+            nc.vector.quantize_mx(
+                out=held["h_codes", b][:, r, :].bitcast(FP8X4),
+                scales=held["h_scales", b][:, r, :],
+                in_=held["hg", r, b][:].rearrange("p c t -> p (c t)"),
+            )
+
+        def attend(b):
+            if not graph(b):
+                return
+            out_rows = out[b].rearrange("(p j) h -> p j h", j=TILES)
+            out_sb = pool2.tile([P, TILES, FEATS], F32, name="out_sb")
             for j in range(TILES):
                 rows = slice(j * P, (j + 1) * P)
                 g = []
                 for r in range(RELS):
-                    g_r = psum_g.tile([P, FEATS], F32, name="g_r")
+                    g_r = psum.tile([P, FEATS], F32, name="g_r", tag="bank")
                     nc.tensor.matmul_mx(
                         out=g_r[:],
-                        lhsT=att_codes[:, r, rows].bitcast(FP8X4),
-                        lhsT_scale=att_scales[:, r, rows],
-                        rhs=h_codes[:, r, :].bitcast(FP8X4),
-                        rhs_scale=h_scales[:, r, :],
+                        lhsT=held["att_codes", b][:, r, rows].bitcast(FP8X4),
+                        lhsT_scale=held["att_scales", b][:, r, rows],
+                        rhs=held["h_codes", b][:, r, :].bitcast(FP8X4),
+                        rhs_scale=held["h_scales", b][:, r, :],
                         start=True,
                         stop=True,
                     )
                     g.append(g_r)
-                relu0 = stats.tile([P, FEATS], F32, name="relu0")
+                relu0 = pool3.tile([P, FEATS], F32, name="relu0")
                 nc.scalar.activation(out=relu0[:], in_=g[0][:], func=FUNC.Relu)
                 nc.vector.scalar_tensor_tensor(
                     out=out_sb[:, j, :],
@@ -223,7 +294,32 @@ def tile_rgat_pa_t_e_kernel(tc, adj, x, dmask, W_words, W_scales, out):
                     op1=ALU.add,
                 )
                 if j % 2 == 1:
-                    nc.gpsimd.dma_start(
-                        out=out[b].rearrange("(p j) h -> p j h", j=TILES)[:, j - 1 : j + 1, :],
-                        in_=out_sb[:, j - 1 : j + 1, :],
-                    )
+                    nc.sync.dma_start(out=out_rows[:, j - 1 : j + 1, :], in_=out_sb[:, j - 1 : j + 1, :])
+
+        load_x(0)
+        load_weight()
+        for i in range(-3, GRAPHS):
+            load_adj(i + 3)
+            load_x(i + 4)
+            exponentials(i + 1)
+            normalise(i)
+            spread_mask(i + 2)
+            transpose_att(i)
+            copy_att(i, 1, 0, nc.scalar.copy)
+            copy_att(i, 1, 1, nc.scalar.copy)
+            add_mask(i + 2)
+            copy_att(i, 0, 0, nc.vector.tensor_copy)
+            fold(i + 2, 1)
+            copy_att(i, 0, 1, nc.vector.tensor_copy)
+            fold(i + 2, 2)
+            transpose_x(i + 3, 0)
+            project(i + 2, 0)
+            quantise_h(i + 2, 0)
+            fold(i + 2, 3)
+            quantise_att(i, 0)
+            reduce_max(i + 2)
+            quantise_att(i, 1)
+            transpose_x(i + 3, 1)
+            project(i + 2, 1)
+            quantise_h(i + 2, 1)
+            attend(i)

@@ -20,8 +20,8 @@ RELS = 2
 P = 128
 PACK = 4
 TILES = NODES // P
+STEPS = GRAPHS * TILES
 BIG = 1.0e30
-FOLDS = 3
 
 FLOPS = 2 * GRAPHS * RELS * NODES * FEATS * FEATS + 2 * GRAPHS * RELS * NODES * NODES * FEATS
 
@@ -30,14 +30,19 @@ def tile_rgat_pa_t_e_kernel(tc, adj, x, dmask, W_words, W_scales, out):
     nc = tc.nc
     with ExitStack() as stack:
         consts = stack.enter_context(tc.tile_pool(name="consts", bufs=1))
+        loads = stack.enter_context(tc.tile_pool(name="loads", bufs=GRAPHS))
         pool2 = stack.enter_context(tc.tile_pool(name="pool2", bufs=2))
         pool3 = stack.enter_context(tc.tile_pool(name="pool3", bufs=3))
         psum = stack.enter_context(tc.psum_pool(name="psum", bufs=8))
+        stack.enter_context(tc.manual_schedule())
 
         held = {}
 
         def graph(b):
             return 0 <= b < GRAPHS
+
+        def row_tile(q):
+            return 0 <= q < STEPS
 
         ident = consts.tile([P, P], F32)
         make_identity(nc, ident[:])
@@ -45,17 +50,13 @@ def tile_rgat_pa_t_e_kernel(tc, adj, x, dmask, W_words, W_scales, out):
         make_identity(nc, ident_bf[:])
         w_codes = consts.tile([P, RELS, FEATS], U32, align_bytes=64)
         w_scales = consts.tile([P, RELS, FEATS], U8, align_bytes=64)
-        nc.vector.memset(w_scales[:].bitcast(I32), 0)
         mask_rows = consts.tile([P, NODES], BF16)
         nc.vector.memset(mask_rows[:], 0.0)
-        nc.sync.dma_start(out=mask_rows[0:GRAPHS, :], in_=dmask.rearrange("b o m -> (b o) m"))
+        nc.vector.memset(w_scales[:].bitcast(I32), 0)
         neg_rows = consts.tile([P, NODES], BF16)
-        nc.vector.tensor_scalar(out=neg_rows[:], in0=mask_rows[:], scalar1=BIG, scalar2=-BIG, op0=ALU.mult, op1=ALU.add)
 
         def load_x(b):
-            if not graph(b):
-                return
-            x_sb = pool2.tile([P, PACK, FEATS], BF16, name="x_sb")
+            x_sb = loads.tile([P, PACK, FEATS], BF16, name="x_sb")
             nc.sync.dma_start(
                 out=x_sb[:].rearrange("p (u e) k -> p u e k", u=2),
                 in_=x[b].rearrange("(u p e) k -> p u e k", u=2, e=2),
@@ -73,12 +74,26 @@ def tile_rgat_pa_t_e_kernel(tc, adj, x, dmask, W_words, W_scales, out):
                 in_=W_words.rearrange("g p n t -> p g (n t)").bitcast(I32),
             )
 
-        def load_adj(b):
-            if not graph(b):
-                return
-            adj_sb = pool3.tile([P, TILES, NODES * RELS], BF16, name="adj_sb")
-            nc.sync.dma_start(out=adj_sb[:], in_=adj[b].rearrange("(p j) m r -> p j (m r)", j=TILES))
-            held["level", 0, b] = adj_sb
+        def load_adj(b, first, last):
+            if first == 0:
+                held["adj", b] = loads.tile([P, TILES, NODES * RELS], BF16, name="adj_sb")
+            nc.sync.dma_start(
+                out=held["adj", b][:, first:last, :],
+                in_=adj[b].rearrange("(p j) m r -> p j (m r)", j=TILES)[:, first:last, :],
+            )
+
+        nc.sync.dma_start(out=mask_rows[0:GRAPHS, :], in_=dmask.rearrange("b o m -> (b o) m"))
+        load_adj(0, 0, 2)
+        load_x(0)
+        load_weight()
+        load_adj(0, 2, 4)
+        load_adj(1, 0, 4)
+        load_x(1)
+        for b in range(2, GRAPHS):
+            load_adj(b, 0, 4)
+            load_x(b)
+
+        nc.vector.tensor_scalar(out=neg_rows[:], in0=mask_rows[:], scalar1=BIG, scalar2=-BIG, op0=ALU.mult, op1=ALU.add)
 
         def spread_mask(b):
             if not graph(b):
@@ -95,231 +110,311 @@ def tile_rgat_pa_t_e_kernel(tc, adj, x, dmask, W_words, W_scales, out):
                 )
             held["neg", b] = neg
 
-        def add_mask(b):
+        def add_mask(b, first, last):
             if not graph(b):
                 return
-            adj_sb = held["level", 0, b]
+            rows = held["adj", b][:, first:last, :]
             nc.vector.tensor_tensor(
-                out=adj_sb[:],
-                in0=adj_sb[:],
-                in1=held["neg", b][:].rearrange("p m r -> p (m r)").unsqueeze(1).to_broadcast([P, TILES, NODES * RELS]),
+                out=rows,
+                in0=rows,
+                in1=held["neg", b][:].rearrange("p m r -> p (m r)").unsqueeze(1).to_broadcast([P, last - first, NODES * RELS]),
                 op=ALU.add,
             )
+            if first == 0:
+                held["negmax", b] = pool3.tile([P, TILES, RELS], F32, name="negmax")
 
-        def fold(b, level):
+        def fold(b, first, last, level):
             if not graph(b):
                 return
             width = (NODES * RELS) >> level
-            before = held["level", level - 1, b]
-            after = pool2.tile([P, TILES, width], BF16, name="fold%d" % level)
-            nc.vector.tensor_tensor(out=after[:], in0=before[:, :, 0:width], in1=before[:, :, width : 2 * width], op=ALU.max)
-            held["level", level, b] = after
+            before = held["adj", b] if level == 1 else held["fold", level - 1, b]
+            if first == 0:
+                held["fold", level, b] = pool2.tile([P, TILES, width], BF16, name="fold%d" % level)
+            rows = slice(first, last)
+            nc.vector.tensor_tensor(
+                out=held["fold", level, b][:, rows, :],
+                in0=before[:, rows, 0:width],
+                in1=before[:, rows, width : 2 * width],
+                op=ALU.max,
+            )
 
-        def reduce_max(b):
+        def reduce_max(b, first, last):
             if not graph(b):
                 return
-            negmax = pool3.tile([P, TILES, RELS], F32, name="negmax")
             nc.vector.tensor_reduce(
-                out=negmax[:],
-                in_=held["level", FOLDS, b][:].rearrange("p j (m r) -> p j r m", r=RELS),
+                out=held["negmax", b][:, first:last, :],
+                in_=held["fold", 3, b][:, first:last, :].rearrange("p j (m r) -> p j r m", r=RELS),
                 axis=AXIS.X,
                 op=ALU.max,
                 negate=True,
             )
-            held["negmax", b] = negmax
 
-        def exponentials(b):
-            if not graph(b):
+        def exponentials(q, r):
+            if not row_tile(q):
                 return
-            logits = held["level", 0, b]
-            negmax = held["negmax", b]
-            e = pool2.tile([P, TILES, RELS, NODES], F32, name="e")
-            sums = pool3.tile([P, TILES, RELS], F32, name="sums")
-            for j in range(TILES):
-                by_rel = logits[:, j, :].rearrange("p (m r) -> p r m", r=RELS)
-                for r in range(RELS):
-                    nc.scalar.activation(
-                        out=e[:, j, r, :],
-                        in_=by_rel[:, r, :],
-                        func=FUNC.Exp,
-                        bias=negmax[:, j, r : r + 1],
-                        scale=1.0,
-                        accum_out=sums[:, j, r : r + 1],
-                    )
-            held["e", b] = e
-            held["sums", b] = sums
-
-        def normalise(b):
-            if not graph(b):
-                return
-            e = held["e", b]
-            recip = pool2.tile([P, TILES, RELS], F32, name="recip")
-            nc.vector.reciprocal(out=recip[:], in_=held["sums", b][:])
-            att = pool2.tile([P, TILES, RELS, NODES], BF16, name="att")
-            for j in range(TILES):
-                for r in range(RELS):
-                    nc.vector.tensor_scalar(
-                        out=att[:, j, r, :],
-                        in0=e[:, j, r, :],
-                        scalar1=recip[:, j, r : r + 1],
-                        scalar2=None,
-                        op0=ALU.mult,
-                    )
-            held["att", b] = att
-
-        def transpose_att(b):
-            if not graph(b):
-                return
-            att = held["att", b]
-            held["attg", b] = pool2.tile([P, RELS, TILES, P, PACK], BF16, name="attg", align_bytes=64)
-            for half in range(2):
-                for r in range(RELS):
-                    aT = psum.tile([P, 2, 2, P], F32, name="aT", tag="bank")
-                    for jj in range(2):
-                        words = att[:, 2 * half + jj, r, :].bitcast(F32)
-                        for u in range(2):
-                            nc.tensor.transpose(aT[:, jj, u, :], words[:, u * P : (u + 1) * P], ident[:])
-                    held["aT", half, r, b] = aT
-
-        def copy_att(b, half, r, copy_out):
-            if not graph(b):
-                return
-            copy_out(
-                out=held["attg", b][:, r, 2 * half : 2 * half + 2, :, :].bitcast(F32),
-                in_=held["aT", half, r, b][:].rearrange("p jj u n -> p jj n u"),
+            b, j = divmod(q, TILES)
+            if r == 0:
+                held["e", q] = pool3.tile([P, RELS, NODES], F32, name="e")
+                held["sums", q] = pool3.tile([P, RELS], F32, name="sums")
+            nc.scalar.activation(
+                out=held["e", q][:, r, :],
+                in_=held["adj", b][:, j, :].rearrange("p (m r) -> p r m", r=RELS)[:, r, :],
+                func=FUNC.Exp,
+                bias=held["negmax", b][:, j, r : r + 1],
+                scale=1.0,
+                accum_out=held["sums", q][:, r : r + 1],
             )
 
-        def quantise_att(b, r):
-            if not graph(b):
+        def reciprocal(q):
+            if not row_tile(q):
+                return
+            held["recip", q] = pool3.tile([P, RELS], F32, name="recip")
+            nc.vector.reciprocal(out=held["recip", q][:], in_=held["sums", q][:])
+
+        def normalise(q, r):
+            if not row_tile(q):
                 return
             if r == 0:
-                held["att_codes", b] = pool2.tile([P, RELS, NODES], U32, name="att_codes", align_bytes=64)
-                held["att_scales", b] = pool2.tile([P, RELS, NODES], U8, name="att_scales", align_bytes=64)
+                held["att", q] = pool3.tile([P, RELS, NODES], BF16, name="att")
+            nc.vector.tensor_scalar(
+                out=held["att", q][:, r, :],
+                in0=held["e", q][:, r, :],
+                scalar1=held["recip", q][:, r : r + 1],
+                scalar2=None,
+                op0=ALU.mult,
+            )
+
+        def transpose_att(q):
+            if not row_tile(q):
+                return
+            aT = psum.tile([P, RELS, 2, P], F32, name="aT", tag="bank")
+            for r in range(RELS):
+                words = held["att", q][:, r, :].bitcast(F32)
+                for u in range(2):
+                    nc.tensor.transpose(aT[:, r, u, :], words[:, u * P : (u + 1) * P], ident[:])
+            held["aT", q] = aT
+
+        def copy_att(q, copy_out):
+            if not row_tile(q):
+                return
+            held["attg", q] = pool3.tile([P, RELS, P, PACK], BF16, name="attg", align_bytes=64)
+            copy_out(
+                out=held["attg", q][:].bitcast(F32),
+                in_=held["aT", q][:].rearrange("p r u n -> p r n u"),
+            )
+
+        def quantise_att(q):
+            if not row_tile(q):
+                return
+            held["att_codes", q] = pool3.tile([P, RELS, P], U32, name="att_codes", align_bytes=64)
+            held["att_scales", q] = pool3.tile([P, RELS, P], U8, name="att_scales", align_bytes=64)
             nc.vector.quantize_mx(
-                out=held["att_codes", b][:, r, :].bitcast(FP8X4),
-                scales=held["att_scales", b][:, r, :],
-                in_=held["attg", b][:, r, :, :, :].rearrange("p j n t -> p (j n t)"),
+                out=held["att_codes", q][:].rearrange("p r n -> p (r n)").bitcast(FP8X4),
+                scales=held["att_scales", q][:].rearrange("p r n -> p (r n)"),
+                in_=held["attg", q][:].rearrange("p r n t -> p (r n t)"),
             )
 
         def transpose_x(b, half):
             if not graph(b):
                 return
-            x_sb = held["x_sb", b]
-            if half == 0:
-                held["xg", b] = pool2.tile([P, PACK, P, PACK], BF16, name="xg", align_bytes=64)
-            xg = held["xg", b]
             xT = psum.tile([P, 2, 2, P], F32, name="xT", tag="bank")
             for tt in range(2):
-                words = x_sb[:, 2 * half + tt, :].bitcast(F32)
+                words = held["x_sb", b][:, 2 * half + tt, :].bitcast(F32)
                 for v in range(2):
                     nc.tensor.transpose(xT[:, tt, v, :], words[:, v : FEATS // 2 : 2], ident[:])
-            nc.scalar.copy(
-                out=xg[:, 2 * half : 2 * half + 2, :, :].bitcast(F32),
-                in_=xT[:].rearrange("p tt v n -> p tt n v"),
-            )
-            if half == 1:
-                x_codes = pool2.tile([P, NODES], U32, name="x_codes", align_bytes=64)
-                x_scales = pool2.tile([P, NODES], U8, name="x_scales", align_bytes=64)
-                nc.vector.quantize_mx(
-                    out=x_codes[:].bitcast(FP8X4),
-                    scales=x_scales[:],
-                    in_=xg[:].rearrange("p t n k -> p (t n k)"),
-                )
-                held["x_codes", b] = x_codes
-                held["x_scales", b] = x_scales
+            held["xT", b, half] = xT
 
-        def project(b, r):
+        def copy_x(b, half, copy_out):
             if not graph(b):
                 return
-            x_codes = held["x_codes", b]
-            x_scales = held["x_scales", b]
-            hg = pool2.tile([P, FEATS, PACK], BF16, name="hg", align_bytes=64)
-            for c in range(FEATS // P):
-                cols = slice(c * P, (c + 1) * P)
-                hps = psum.tile([P, PACK, P], F32, name="hps", tag="bank")
-                for t in range(PACK):
-                    rows = slice(t * P, (t + 1) * P)
-                    nc.tensor.matmul_mx(
-                        out=hps[:, t, :],
-                        lhsT=x_codes[:, rows].bitcast(FP8X4),
-                        lhsT_scale=x_scales[:, rows],
-                        rhs=w_codes[:, r, cols].bitcast(FP8X4),
-                        rhs_scale=w_scales[:, r, cols],
-                        start=True,
-                        stop=True,
-                    )
-                nc.scalar.copy(out=hg[:, cols, :], in_=hps[:].rearrange("p t c -> p c t"))
-            held["hg", r, b] = hg
+            if half == 0:
+                held["xg", b] = pool2.tile([P, PACK, P, PACK], BF16, name="xg", align_bytes=64)
+            copy_out(
+                out=held["xg", b][:, 2 * half : 2 * half + 2, :, :].bitcast(F32),
+                in_=held["xT", b, half][:].rearrange("p tt v n -> p tt n v"),
+            )
+
+        def quantise_x(b):
+            if not graph(b):
+                return
+            held["x_codes", b] = pool2.tile([P, NODES], U32, name="x_codes", align_bytes=64)
+            held["x_scales", b] = pool2.tile([P, NODES], U8, name="x_scales", align_bytes=64)
+            nc.vector.quantize_mx(
+                out=held["x_codes", b][:].bitcast(FP8X4),
+                scales=held["x_scales", b][:],
+                in_=held["xg", b][:].rearrange("p t n k -> p (t n k)"),
+            )
+
+        def project(b, piece):
+            if not graph(b):
+                return
+            r, c = divmod(piece, PACK)
+            cols = slice(c * P, (c + 1) * P)
+            hps = psum.tile([P, PACK, P], F32, name="hps", tag="bank")
+            for t in range(PACK):
+                rows = slice(t * P, (t + 1) * P)
+                nc.tensor.matmul_mx(
+                    out=hps[:, t, :],
+                    lhsT=held["x_codes", b][:, rows].bitcast(FP8X4),
+                    lhsT_scale=held["x_scales", b][:, rows],
+                    rhs=w_codes[:, r, cols].bitcast(FP8X4),
+                    rhs_scale=w_scales[:, r, cols],
+                    start=True,
+                    stop=True,
+                )
+            held["hps", b, piece] = hps
+
+        def copy_h(b, piece, copy_out):
+            if not graph(b):
+                return
+            r, c = divmod(piece, PACK)
+            if c == 0:
+                held["hg", b, r] = pool2.tile([P, FEATS, PACK], BF16, name="hg", align_bytes=64)
+            copy_out(
+                out=held["hg", b, r][:, c * P : (c + 1) * P, :],
+                in_=held["hps", b, piece][:].rearrange("p t c -> p c t"),
+            )
 
         def quantise_h(b, r):
             if not graph(b):
                 return
             if r == 0:
-                held["h_codes", b] = pool3.tile([P, RELS, FEATS], U32, name="h_codes", align_bytes=64)
-                held["h_scales", b] = pool3.tile([P, RELS, FEATS], U8, name="h_scales", align_bytes=64)
+                held["h_codes", b] = pool2.tile([P, RELS, FEATS], U32, name="h_codes", align_bytes=64)
+                held["h_scales", b] = pool2.tile([P, RELS, FEATS], U8, name="h_scales", align_bytes=64)
             nc.vector.quantize_mx(
                 out=held["h_codes", b][:, r, :].bitcast(FP8X4),
                 scales=held["h_scales", b][:, r, :],
-                in_=held["hg", r, b][:].rearrange("p c t -> p (c t)"),
+                in_=held["hg", b, r][:].rearrange("p c t -> p (c t)"),
             )
 
-        def attend(b):
-            if not graph(b):
+        def attend(q):
+            if not row_tile(q):
                 return
-            out_rows = out[b].rearrange("(p j) h -> p j h", j=TILES)
-            out_sb = pool2.tile([P, TILES, FEATS], F32, name="out_sb")
-            for j in range(TILES):
-                rows = slice(j * P, (j + 1) * P)
-                g = []
-                for r in range(RELS):
-                    g_r = psum.tile([P, FEATS], F32, name="g_r", tag="bank")
-                    nc.tensor.matmul_mx(
-                        out=g_r[:],
-                        lhsT=held["att_codes", b][:, r, rows].bitcast(FP8X4),
-                        lhsT_scale=held["att_scales", b][:, r, rows],
-                        rhs=held["h_codes", b][:, r, :].bitcast(FP8X4),
-                        rhs_scale=held["h_scales", b][:, r, :],
-                        start=True,
-                        stop=True,
-                    )
-                    g.append(g_r)
-                relu0 = pool3.tile([P, FEATS], F32, name="relu0")
-                nc.scalar.activation(out=relu0[:], in_=g[0][:], func=FUNC.Relu)
-                nc.vector.scalar_tensor_tensor(
-                    out=out_sb[:, j, :],
-                    in0=g[1][:],
-                    scalar=0.0,
-                    in1=relu0[:],
-                    op0=ALU.max,
-                    op1=ALU.add,
+            b = q // TILES
+            for r in range(RELS):
+                g_r = psum.tile([P, FEATS], F32, name="g_r", tag="bank")
+                nc.tensor.matmul_mx(
+                    out=g_r[:],
+                    lhsT=held["att_codes", q][:, r, :].bitcast(FP8X4),
+                    lhsT_scale=held["att_scales", q][:, r, :],
+                    rhs=held["h_codes", b][:, r, :].bitcast(FP8X4),
+                    rhs_scale=held["h_scales", b][:, r, :],
+                    start=True,
+                    stop=True,
                 )
-                if j % 2 == 1:
-                    nc.sync.dma_start(out=out_rows[:, j - 1 : j + 1, :], in_=out_sb[:, j - 1 : j + 1, :])
+                held["g", q, r] = g_r
 
-        load_x(0)
-        load_weight()
-        for i in range(-3, GRAPHS):
-            load_adj(i + 3)
-            load_x(i + 4)
-            exponentials(i + 1)
-            normalise(i)
-            spread_mask(i + 2)
-            transpose_att(i)
-            copy_att(i, 1, 0, nc.scalar.copy)
-            copy_att(i, 1, 1, nc.scalar.copy)
-            add_mask(i + 2)
-            copy_att(i, 0, 0, nc.vector.tensor_copy)
-            fold(i + 2, 1)
-            copy_att(i, 0, 1, nc.vector.tensor_copy)
-            fold(i + 2, 2)
-            transpose_x(i + 3, 0)
-            project(i + 2, 0)
-            quantise_h(i + 2, 0)
-            fold(i + 2, 3)
-            quantise_att(i, 0)
-            reduce_max(i + 2)
-            quantise_att(i, 1)
-            transpose_x(i + 3, 1)
-            project(i + 2, 1)
-            quantise_h(i + 2, 1)
-            attend(i)
+        def relu_first(q):
+            if not row_tile(q):
+                return
+            held["relu0", q] = pool3.tile([P, FEATS], F32, name="relu0")
+            nc.scalar.activation(out=held["relu0", q][:], in_=held["g", q, 0][:], func=FUNC.Relu)
+
+        def add_relus(q):
+            if not row_tile(q):
+                return
+            b, j = divmod(q, TILES)
+            if j % 2 == 0:
+                held["out_sb", q // 2] = pool2.tile([P, 2, FEATS], F32, name="out_sb")
+            out_sb = held["out_sb", q // 2]
+            nc.vector.scalar_tensor_tensor(
+                out=out_sb[:, j % 2, :],
+                in0=held["g", q, 1][:],
+                scalar=0.0,
+                in1=held["relu0", q][:],
+                op0=ALU.max,
+                op1=ALU.add,
+            )
+            out_rows = out[b].rearrange("(p j) h -> p j h", j=TILES)
+            if b == GRAPHS - 1:
+                nc.sync.dma_start(out=out_rows[:, j, :], in_=out_sb[:, j % 2, :])
+            elif j % 2 == 1:
+                nc.sync.dma_start(out=out_rows[:, j - 1 : j + 1, :], in_=out_sb[:])
+
+        def h_pieces(s):
+            b, k = divmod(s + 2, TILES)
+            return b, 2 * k
+
+        def step(s):
+            c, k = divmod(s, TILES)
+            ahead = c + 1
+            hb, piece = h_pieces(s)
+            reciprocal(s - 1)
+            if k < 2:
+                copy_att(s - 2, nc.scalar.copy)
+            else:
+                copy_att(s - 2, nc.vector.tensor_copy)
+            exponentials(s, 0)
+            if s == 0:
+                add_mask(0, 2, 4)
+                fold(0, 2, 4, 1)
+                fold(0, 2, 4, 2)
+                fold(0, 2, 4, 3)
+                reduce_max(0, 2, 4)
+                spread_mask(1)
+                exponentials(0, 1)
+                copy_h(0, 0, nc.scalar.copy)
+                copy_h(0, 1, nc.scalar.copy)
+                copy_x(1, 0, nc.scalar.copy)
+                copy_x(1, 1, nc.scalar.copy)
+                copy_h(0, 2, nc.scalar.copy)
+                copy_h(0, 3, nc.scalar.copy)
+                project(0, 4)
+                project(0, 5)
+            if k == 0:
+                add_mask(ahead, 0, 2)
+                quantise_h(c, 0)
+            if k == 1:
+                add_mask(ahead, 2, 4)
+            if k == 2:
+                fold(ahead, 0, 4, 1)
+                quantise_h(c, 1)
+            if k == 3:
+                fold(ahead, 0, 4, 3)
+            normalise(s - 1, 0)
+            normalise(s - 1, 1)
+            relu_first(s - 3)
+            copy_h(hb, piece, nc.scalar.copy)
+            if k == 2:
+                transpose_x(c + 2, 0)
+            if k == 3:
+                transpose_x(c + 2, 1)
+                spread_mask(c + 2)
+            transpose_att(s - 1)
+            quantise_att(s - 2)
+            if k == 2:
+                fold(ahead, 0, 4, 2)
+            if k == 3:
+                reduce_max(ahead, 0, 4)
+            if k == 1:
+                quantise_x(ahead)
+            if s > 0:
+                exponentials(s, 1)
+            copy_h(hb, piece + 1, nc.scalar.copy)
+            add_relus(s - 3)
+            if k == 2:
+                copy_x(c + 2, 0, nc.scalar.copy)
+            if k == 3:
+                copy_x(c + 2, 1, nc.scalar.copy)
+            attend(s - 2)
+            nb, next_piece = h_pieces(s + 1)
+            project(nb, next_piece)
+            project(nb, next_piece + 1)
+
+        spread_mask(0)
+        transpose_x(0, 0)
+        transpose_x(0, 1)
+        add_mask(0, 0, 2)
+        copy_x(0, 0, nc.scalar.copy)
+        copy_x(0, 1, nc.scalar.copy)
+        fold(0, 0, 2, 1)
+        fold(0, 0, 2, 2)
+        fold(0, 0, 2, 3)
+        quantise_x(0)
+        reduce_max(0, 0, 2)
+        for piece in range(4):
+            project(0, piece)
+        transpose_x(1, 0)
+        transpose_x(1, 1)
+        for s in range(STEPS + 3):
+            step(s)

@@ -22,6 +22,7 @@ PACK = 4
 TILES = NODES // P
 STEPS = GRAPHS * TILES
 BIG = 1.0e30
+FOLDS = 5
 
 FLOPS = 2 * GRAPHS * RELS * NODES * FEATS * FEATS + 2 * GRAPHS * RELS * NODES * NODES * FEATS
 
@@ -32,6 +33,7 @@ def tile_rgat_pa_t_e_kernel(tc, adj, x, dmask, W_words, W_scales, out):
         consts = stack.enter_context(tc.tile_pool(name="consts", bufs=1))
         loads = stack.enter_context(tc.tile_pool(name="loads", bufs=GRAPHS))
         pool2 = stack.enter_context(tc.tile_pool(name="pool2", bufs=2))
+        pool4 = stack.enter_context(tc.tile_pool(name="pool4", bufs=4))
         pool3 = stack.enter_context(tc.tile_pool(name="pool3", bufs=3))
         psum = stack.enter_context(tc.psum_pool(name="psum", bufs=8))
         stack.enter_context(tc.manual_schedule())
@@ -83,8 +85,8 @@ def tile_rgat_pa_t_e_kernel(tc, adj, x, dmask, W_words, W_scales, out):
             )
 
         nc.sync.dma_start(out=mask_rows[0:GRAPHS, :], in_=dmask.rearrange("b o m -> (b o) m"))
-        load_adj(0, 0, 2)
         load_x(0)
+        load_adj(0, 0, 2)
         load_weight()
         load_adj(0, 2, 4)
         load_adj(1, 0, 4)
@@ -138,12 +140,12 @@ def tile_rgat_pa_t_e_kernel(tc, adj, x, dmask, W_words, W_scales, out):
                 op=ALU.max,
             )
 
-        def reduce_max(b, first, last):
+        def reduce_max(b, first, last, level):
             if not graph(b):
                 return
             nc.vector.tensor_reduce(
                 out=held["negmax", b][:, first:last, :],
-                in_=held["fold", 3, b][:, first:last, :].rearrange("p j (m r) -> p j r m", r=RELS),
+                in_=held["fold", level, b][:, first:last, :].rearrange("p j (m r) -> p j r m", r=RELS),
                 axis=AXIS.X,
                 op=ALU.max,
                 negate=True,
@@ -154,7 +156,7 @@ def tile_rgat_pa_t_e_kernel(tc, adj, x, dmask, W_words, W_scales, out):
                 return
             b, j = divmod(q, TILES)
             if r == 0:
-                held["e", q] = pool3.tile([P, RELS, NODES], F32, name="e")
+                held["e", q] = pool4.tile([P, RELS, NODES], F32, name="e")
                 held["sums", q] = pool3.tile([P, RELS], F32, name="sums")
             nc.scalar.activation(
                 out=held["e", q][:, r, :],
@@ -174,7 +176,7 @@ def tile_rgat_pa_t_e_kernel(tc, adj, x, dmask, W_words, W_scales, out):
         def normalise(q, r):
             if not row_tile(q):
                 return
-            if r == 0:
+            if ("att", q) not in held:
                 held["att", q] = pool3.tile([P, RELS, NODES], BF16, name="att")
             nc.vector.tensor_scalar(
                 out=held["att", q][:, r, :],
@@ -337,69 +339,65 @@ def tile_rgat_pa_t_e_kernel(tc, adj, x, dmask, W_words, W_scales, out):
 
         def step(s):
             c, k = divmod(s, TILES)
-            ahead = c + 1
             hb, piece = h_pieces(s)
-            reciprocal(s - 1)
-            if k < 2:
-                copy_att(s - 2, nc.scalar.copy)
-            else:
-                copy_att(s - 2, nc.vector.tensor_copy)
-            exponentials(s, 0)
-            if s == 0:
-                add_mask(0, 2, 4)
-                fold(0, 2, 4, 1)
-                fold(0, 2, 4, 2)
-                fold(0, 2, 4, 3)
-                reduce_max(0, 2, 4)
-                spread_mask(1)
-                exponentials(0, 1)
-                copy_h(0, 0, nc.scalar.copy)
-                copy_h(0, 1, nc.scalar.copy)
-                copy_x(1, 0, nc.scalar.copy)
-                copy_x(1, 1, nc.scalar.copy)
-                copy_h(0, 2, nc.scalar.copy)
-                copy_h(0, 3, nc.scalar.copy)
-                project(0, 4)
-                project(0, 5)
+            normalise(s - 2, 0)
+            normalise(s - 2, 1)
+            if s > 0:
+                exponentials(s, 0)
+            if k == 2:
+                fold(c + 1, 0, 4, 2)
+            transpose_att(s - 2)
+            if k == 3:
+                transpose_x(c + 2, 0)
             if k == 0:
-                add_mask(ahead, 0, 2)
+                transpose_x(c + 1, 1)
+            if k == 2:
+                spread_mask(c + 2)
+            quantise_att(s - 3)
+            if k == 2:
+                fold(c + 1, 0, 4, 3)
+            if k == 0:
                 quantise_h(c, 0)
             if k == 1:
-                add_mask(ahead, 2, 4)
+                quantise_x(c + 1)
             if k == 2:
-                fold(ahead, 0, 4, 1)
                 quantise_h(c, 1)
-            if k == 3:
-                fold(ahead, 0, 4, 3)
-            normalise(s - 1, 0)
-            normalise(s - 1, 1)
-            relu_first(s - 3)
+            relu_first(s - 4)
             copy_h(hb, piece, nc.scalar.copy)
-            if k == 2:
-                transpose_x(c + 2, 0)
-            if k == 3:
-                transpose_x(c + 2, 1)
-                spread_mask(c + 2)
-            transpose_att(s - 1)
-            quantise_att(s - 2)
-            if k == 2:
-                fold(ahead, 0, 4, 2)
-            if k == 3:
-                reduce_max(ahead, 0, 4)
-            if k == 1:
-                quantise_x(ahead)
             if s > 0:
                 exponentials(s, 1)
-            copy_h(hb, piece + 1, nc.scalar.copy)
-            add_relus(s - 3)
-            if k == 2:
-                copy_x(c + 2, 0, nc.scalar.copy)
-            if k == 3:
-                copy_x(c + 2, 1, nc.scalar.copy)
-            attend(s - 2)
+            attend(s - 3)
             nb, next_piece = h_pieces(s + 1)
             project(nb, next_piece)
             project(nb, next_piece + 1)
+            if k == 1:
+                fold(c + 1, 0, 4, 1)
+            if k == 2:
+                fold(c + 1, 0, 4, 4)
+            reciprocal(s - 1)
+            if k == 2:
+                fold(c + 1, 0, 4, 5)
+            if k == 3:
+                add_mask(c + 2, 0, 2)
+            if k == 0:
+                add_mask(c + 1, 2, 4)
+            if k == 1 or k == 2 or s >= STEPS:
+                copy_att(s - 2, nc.scalar.copy)
+            else:
+                copy_att(s - 2, nc.vector.tensor_copy)
+            copy_h(hb, piece + 1, nc.scalar.copy)
+            add_relus(s - 4)
+            if k == 2:
+                reduce_max(c + 1, 0, 4, FOLDS)
+            if k == 3:
+                copy_x(c + 2, 0, nc.scalar.copy)
+            if k == 0:
+                copy_x(c + 1, 1, nc.scalar.copy)
+
+        def head_maximum(first, last):
+            fold(0, first, last, 1)
+            fold(0, first, last, 2)
+            reduce_max(0, first, last, 2)
 
         spread_mask(0)
         transpose_x(0, 0)
@@ -407,14 +405,21 @@ def tile_rgat_pa_t_e_kernel(tc, adj, x, dmask, W_words, W_scales, out):
         add_mask(0, 0, 2)
         copy_x(0, 0, nc.scalar.copy)
         copy_x(0, 1, nc.scalar.copy)
-        fold(0, 0, 2, 1)
-        fold(0, 0, 2, 2)
-        fold(0, 0, 2, 3)
+        head_maximum(0, 2)
         quantise_x(0)
-        reduce_max(0, 0, 2)
         for piece in range(4):
             project(0, piece)
+        spread_mask(1)
         transpose_x(1, 0)
-        transpose_x(1, 1)
-        for s in range(STEPS + 3):
+        exponentials(0, 0)
+        exponentials(0, 1)
+        add_mask(0, 2, 4)
+        head_maximum(2, 4)
+        for piece in range(4):
+            copy_h(0, piece, nc.scalar.copy)
+        copy_x(1, 0, nc.scalar.copy)
+        add_mask(1, 0, 2)
+        project(0, 4)
+        project(0, 5)
+        for s in range(STEPS + 4):
             step(s)

@@ -173,17 +173,18 @@ def tile_rgat_pa_t_e_kernel(tc, adj, x, dmask, W_words, W_scales, out):
             held["recip", q] = pool3.tile([P, RELS], F32, name="recip")
             nc.vector.reciprocal(out=held["recip", q][:], in_=held["sums", q][:])
 
-        def normalise(q, r):
+        def normalise(q, r, engine):
             if not row_tile(q):
                 return
             if ("att", q) not in held:
                 held["att", q] = pool3.tile([P, RELS, NODES], BF16, name="att")
-            nc.vector.tensor_scalar(
+            engine.tensor_scalar(
                 out=held["att", q][:, r, :],
                 in0=held["e", q][:, r, :],
                 scalar1=held["recip", q][:, r : r + 1],
-                scalar2=None,
+                scalar2=1.0,
                 op0=ALU.mult,
+                op1=ALU.mult,
             )
 
         def transpose_att(q):
@@ -337,11 +338,15 @@ def tile_rgat_pa_t_e_kernel(tc, adj, x, dmask, W_words, W_scales, out):
             b, k = divmod(s + 2, TILES)
             return b, 2 * k
 
+        def on_gpsimd(q, r):
+            return (r == 1 or (q + 1) % TILES in (3, 0)) and q < STEPS - 4
+
         def step(s):
             c, k = divmod(s, TILES)
             hb, piece = h_pieces(s)
-            normalise(s - 2, 0)
-            normalise(s - 2, 1)
+            for r in range(RELS):
+                if not on_gpsimd(s - 2, r):
+                    normalise(s - 2, r, nc.vector)
             if s > 0:
                 exponentials(s, 0)
             if k == 2:
@@ -377,11 +382,14 @@ def tile_rgat_pa_t_e_kernel(tc, adj, x, dmask, W_words, W_scales, out):
             reciprocal(s - 1)
             if k == 2:
                 fold(c + 1, 0, 4, 5)
+            for r in range(RELS):
+                if on_gpsimd(s - 1, r):
+                    normalise(s - 1, r, nc.gpsimd)
             if k == 3:
                 add_mask(c + 2, 0, 2)
             if k == 0:
                 add_mask(c + 1, 2, 4)
-            if k == 1 or k == 2 or s >= STEPS:
+            if k == 2 or s >= STEPS:
                 copy_att(s - 2, nc.scalar.copy)
             else:
                 copy_att(s - 2, nc.vector.tensor_copy)

@@ -22,7 +22,7 @@ PACK = 4
 TILES = NODES // P
 STEPS = GRAPHS * TILES
 BIG = 1.0e30
-FOLDS = 5
+FOLDS = 4
 
 FLOPS = 2 * GRAPHS * RELS * NODES * FEATS * FEATS + 2 * GRAPHS * RELS * NODES * NODES * FEATS
 
@@ -35,7 +35,7 @@ def tile_rgat_pa_t_e_kernel(tc, adj, x, dmask, W_words, W_scales, out):
         pool2 = stack.enter_context(tc.tile_pool(name="pool2", bufs=2))
         pool4 = stack.enter_context(tc.tile_pool(name="pool4", bufs=4))
         pool3 = stack.enter_context(tc.tile_pool(name="pool3", bufs=3))
-        psum = stack.enter_context(tc.psum_pool(name="psum", bufs=8))
+        psum = stack.enter_context(tc.psum_pool(name="psum", bufs=4))
         stack.enter_context(tc.manual_schedule())
 
         held = {}
@@ -85,12 +85,12 @@ def tile_rgat_pa_t_e_kernel(tc, adj, x, dmask, W_words, W_scales, out):
             )
 
         nc.sync.dma_start(out=mask_rows[0:GRAPHS, :], in_=dmask.rearrange("b o m -> (b o) m"))
-        load_x(0)
         load_adj(0, 0, 2)
+        load_x(0)
+        load_x(1)
         load_weight()
         load_adj(0, 2, 4)
         load_adj(1, 0, 4)
-        load_x(1)
         for b in range(2, GRAPHS):
             load_adj(b, 0, 4)
             load_x(b)
@@ -100,7 +100,7 @@ def tile_rgat_pa_t_e_kernel(tc, adj, x, dmask, W_words, W_scales, out):
         def spread_mask(b):
             if not graph(b):
                 return
-            neg = psum.tile([P, NODES, RELS], BF16, name="neg", tag="bank")
+            neg = psum.tile([P, NODES, RELS], BF16, name="neg", bufs=2)
             for half in range(2):
                 keys = slice(half * NODES // 2, (half + 1) * NODES // 2)
                 nc.tensor.matmul(
@@ -122,7 +122,7 @@ def tile_rgat_pa_t_e_kernel(tc, adj, x, dmask, W_words, W_scales, out):
                 in1=held["neg", b][:].rearrange("p m r -> p (m r)").unsqueeze(1).to_broadcast([P, last - first, NODES * RELS]),
                 op=ALU.add,
             )
-            if first == 0:
+            if ("negmax", b) not in held:
                 held["negmax", b] = pool3.tile([P, TILES, RELS], F32, name="negmax")
 
         def fold(b, first, last, level):
@@ -130,7 +130,7 @@ def tile_rgat_pa_t_e_kernel(tc, adj, x, dmask, W_words, W_scales, out):
                 return
             width = (NODES * RELS) >> level
             before = held["adj", b] if level == 1 else held["fold", level - 1, b]
-            if first == 0:
+            if ("fold", level, b) not in held:
                 held["fold", level, b] = pool2.tile([P, TILES, width], BF16, name="fold%d" % level)
             rows = slice(first, last)
             nc.vector.tensor_tensor(
@@ -173,19 +173,19 @@ def tile_rgat_pa_t_e_kernel(tc, adj, x, dmask, W_words, W_scales, out):
             held["recip", q] = pool3.tile([P, RELS], F32, name="recip")
             nc.vector.reciprocal(out=held["recip", q][:], in_=held["sums", q][:])
 
-        def normalise(q, r, engine):
+        def normalise(q, engine):
             if not row_tile(q):
                 return
-            if ("att", q) not in held:
-                held["att", q] = pool3.tile([P, RELS, NODES], BF16, name="att")
-            engine.tensor_scalar(
-                out=held["att", q][:, r, :],
-                in0=held["e", q][:, r, :],
-                scalar1=held["recip", q][:, r : r + 1],
-                scalar2=1.0,
-                op0=ALU.mult,
-                op1=ALU.mult,
-            )
+            held["att", q] = pool3.tile([P, RELS, NODES], BF16, name="att")
+            for r in range(RELS):
+                engine.tensor_scalar(
+                    out=held["att", q][:, r, :],
+                    in0=held["e", q][:, r, :],
+                    scalar1=held["recip", q][:, r : r + 1],
+                    scalar2=1.0,
+                    op0=ALU.mult,
+                    op1=ALU.mult,
+                )
 
         def transpose_att(q):
             if not row_tile(q):
@@ -240,8 +240,8 @@ def tile_rgat_pa_t_e_kernel(tc, adj, x, dmask, W_words, W_scales, out):
         def quantise_x(b):
             if not graph(b):
                 return
-            held["x_codes", b] = pool2.tile([P, NODES], U32, name="x_codes", align_bytes=64)
-            held["x_scales", b] = pool2.tile([P, NODES], U8, name="x_scales", align_bytes=64)
+            held["x_codes", b] = pool3.tile([P, NODES], U32, name="x_codes", align_bytes=64)
+            held["x_scales", b] = pool3.tile([P, NODES], U8, name="x_scales", align_bytes=64)
             nc.vector.quantize_mx(
                 out=held["x_codes", b][:].bitcast(FP8X4),
                 scales=held["x_scales", b][:],
@@ -253,7 +253,7 @@ def tile_rgat_pa_t_e_kernel(tc, adj, x, dmask, W_words, W_scales, out):
                 return
             r, c = divmod(piece, PACK)
             cols = slice(c * P, (c + 1) * P)
-            hps = psum.tile([P, PACK, P], F32, name="hps", tag="bank")
+            hps = psum.tile([P, PACK, P], F32, name="hps", bufs=2)
             for t in range(PACK):
                 rows = slice(t * P, (t + 1) * P)
                 nc.tensor.matmul_mx(
@@ -272,7 +272,7 @@ def tile_rgat_pa_t_e_kernel(tc, adj, x, dmask, W_words, W_scales, out):
                 return
             r, c = divmod(piece, PACK)
             if c == 0:
-                held["hg", b, r] = pool2.tile([P, FEATS, PACK], BF16, name="hg", align_bytes=64)
+                held["hg", b, r] = pool3.tile([P, FEATS, PACK], BF16, name="hg", align_bytes=64)
             copy_out(
                 out=held["hg", b, r][:, c * P : (c + 1) * P, :],
                 in_=held["hps", b, piece][:].rearrange("p t c -> p c t"),
@@ -338,96 +338,105 @@ def tile_rgat_pa_t_e_kernel(tc, adj, x, dmask, W_words, W_scales, out):
             b, k = divmod(s + 2, TILES)
             return b, 2 * k
 
-        def on_gpsimd(q, r):
-            return (r == 1 or (q + 1) % TILES in (3, 0)) and q < STEPS - 4
+        def on_gpsimd(q):
+            return 1 < q < STEPS - 4
+
+        def half_graph(half):
+            b, side = divmod(half, 2)
+            return b, 2 * side
 
         def step(s):
             c, k = divmod(s, TILES)
+            i, odd = divmod(s, 2)
             hb, piece = h_pieces(s)
-            for r in range(RELS):
-                if not on_gpsimd(s - 2, r):
-                    normalise(s - 2, r, nc.vector)
+            b, first = half_graph(i + 1)
+            b2, first2 = half_graph(i + 2)
             if s > 0:
                 exponentials(s, 0)
-            if k == 2:
-                fold(c + 1, 0, 4, 2)
             transpose_att(s - 2)
             if k == 3:
-                transpose_x(c + 2, 0)
-            if k == 0:
-                transpose_x(c + 1, 1)
-            if k == 2:
                 spread_mask(c + 2)
-            quantise_att(s - 3)
-            if k == 2:
-                fold(c + 1, 0, 4, 3)
-            if k == 0:
-                quantise_h(c, 0)
-            if k == 1:
-                quantise_x(c + 1)
-            if k == 2:
-                quantise_h(c, 1)
+            if k == 1 or k == 2:
+                transpose_x(c + 2, k - 1)
+            reciprocal(s - 1)
             relu_first(s - 4)
             copy_h(hb, piece, nc.scalar.copy)
-            if s > 0:
-                exponentials(s, 1)
+            if not on_gpsimd(s - 1):
+                normalise(s - 1, nc.vector)
+            quantise_att(s - 3)
             attend(s - 3)
             nb, next_piece = h_pieces(s + 1)
             project(nb, next_piece)
             project(nb, next_piece + 1)
-            if k == 1:
-                fold(c + 1, 0, 4, 1)
-            if k == 2:
-                fold(c + 1, 0, 4, 4)
-            reciprocal(s - 1)
-            if k == 2:
-                fold(c + 1, 0, 4, 5)
-            for r in range(RELS):
-                if on_gpsimd(s - 1, r):
-                    normalise(s - 1, r, nc.gpsimd)
-            if k == 3:
-                add_mask(c + 2, 0, 2)
-            if k == 0:
-                add_mask(c + 1, 2, 4)
-            if k == 2 or s >= STEPS:
-                copy_att(s - 2, nc.scalar.copy)
-            else:
-                copy_att(s - 2, nc.vector.tensor_copy)
-            copy_h(hb, piece + 1, nc.scalar.copy)
+            if odd:
+                fold(b, first, first + 2, 4)
+            if on_gpsimd(s - 1):
+                normalise(s - 1, nc.gpsimd)
+            add_mask(b2, first2 + odd, first2 + odd + 1)
+            if odd:
+                reduce_max(b, first, first + 2, FOLDS)
+            copy_att(s - 2, nc.vector.tensor_copy)
+            if s > 0:
+                exponentials(s, 1)
             add_relus(s - 4)
-            if k == 2:
-                reduce_max(c + 1, 0, 4, FOLDS)
-            if k == 3:
-                copy_x(c + 2, 0, nc.scalar.copy)
+            if not odd:
+                fold(b, first, first + 2, 2)
+            else:
+                fold(b2, first2, first2 + 2, 1)
+            copy_h(hb, piece + 1, nc.scalar.copy)
+            if k == 1 or k == 2:
+                quantise_h(c, k - 1)
+                copy_x(c + 2, k - 1, nc.scalar.copy)
             if k == 0:
-                copy_x(c + 1, 1, nc.scalar.copy)
-
-        def head_maximum(first, last):
-            fold(0, first, last, 1)
-            fold(0, first, last, 2)
-            reduce_max(0, first, last, 2)
+                quantise_x(c + 1)
+            if not odd:
+                fold(b, first, first + 2, 3)
 
         spread_mask(0)
-        transpose_x(0, 0)
-        transpose_x(0, 1)
+        for half in range(2):
+            transpose_x(0, half)
+        spread_mask(1)
+        for half in range(2):
+            transpose_x(1, half)
         add_mask(0, 0, 2)
-        copy_x(0, 0, nc.scalar.copy)
-        copy_x(0, 1, nc.scalar.copy)
-        head_maximum(0, 2)
+        for half in range(2):
+            copy_x(0, half, nc.scalar.copy)
+        for half in range(2):
+            copy_x(1, half, nc.scalar.copy)
+        fold(0, 0, 2, 1)
+        fold(0, 0, 2, 2)
+        reduce_max(0, 0, 2, 2)
         quantise_x(0)
         for piece in range(4):
             project(0, piece)
-        spread_mask(1)
-        transpose_x(1, 0)
         exponentials(0, 0)
         exponentials(0, 1)
         add_mask(0, 2, 4)
-        head_maximum(2, 4)
+        fold(0, 2, 4, 1)
         for piece in range(4):
             copy_h(0, piece, nc.scalar.copy)
-        copy_x(1, 0, nc.scalar.copy)
-        add_mask(1, 0, 2)
         project(0, 4)
         project(0, 5)
-        for s in range(STEPS + 4):
+        for s in range(STEPS):
             step(s)
+        last = STEPS - 1
+        reciprocal(last)
+        for q in (last - 1, last):
+            normalise(q, nc.vector)
+            transpose_att(q)
+        quantise_att(last - 2)
+        relu_first(last - 3)
+        attend(last - 2)
+        add_relus(last - 3)
+        copy_att(last - 1, nc.scalar.copy)
+        quantise_att(last - 1)
+        attend(last - 1)
+        copy_att(last, nc.scalar.copy)
+        relu_first(last - 2)
+        quantise_att(last)
+        attend(last)
+        add_relus(last - 2)
+        relu_first(last - 1)
+        add_relus(last - 1)
+        relu_first(last)
+        add_relus(last)

@@ -56,6 +56,8 @@ def tile_rgat_pa_t_e_kernel(tc, adj, x, dmask, W_words, W_scales, out):
         nc.vector.memset(mask_rows[:], 0.0)
         nc.vector.memset(w_scales[:].bitcast(I32), 0)
         neg_rows = consts.tile([P, NODES], BF16)
+        warm_rows = consts.tile([P, NODES], BF16)
+        nc.vector.memset(warm_rows[:], 0.0)
 
         def load_x(b):
             x_sb = loads.tile([P, PACK, FEATS], BF16, name="x_sb")
@@ -96,6 +98,11 @@ def tile_rgat_pa_t_e_kernel(tc, adj, x, dmask, W_words, W_scales, out):
             load_x(b)
 
         nc.vector.tensor_scalar(out=neg_rows[:], in0=mask_rows[:], scalar1=BIG, scalar2=-BIG, op0=ALU.mult, op1=ALU.add)
+
+        def keep_warm(count):
+            for i in range(count):
+                idle = psum.tile([P, NODES], F32, name="idle", tag="bank")
+                nc.tensor.matmul(out=idle[:], lhsT=warm_rows[:, 0:P], rhs=warm_rows[:], start=True, stop=True)
 
         def spread_mask(b):
             if not graph(b):
@@ -186,6 +193,22 @@ def tile_rgat_pa_t_e_kernel(tc, adj, x, dmask, W_words, W_scales, out):
                     op0=ALU.mult,
                     op1=ALU.mult,
                 )
+
+        def normalise_on_two(q):
+            held["att", q] = pool3.tile([P, RELS, NODES], BF16, name="att")
+            nc.vector.tensor_scalar(
+                out=held["att", q][:, 0, :],
+                in0=held["e", q][:, 0, :],
+                scalar1=held["recip", q][:, 0:1],
+                scalar2=None,
+                op0=ALU.mult,
+            )
+            nc.scalar.activation(
+                out=held["att", q][:, 1, :],
+                in_=held["e", q][:, 1, :],
+                func=FUNC.Copy,
+                scale=held["recip", q][:, 1:2],
+            )
 
         def transpose_att(q):
             if not row_tile(q):
@@ -278,16 +301,17 @@ def tile_rgat_pa_t_e_kernel(tc, adj, x, dmask, W_words, W_scales, out):
                 in_=held["hps", b, piece][:].rearrange("p t c -> p c t"),
             )
 
-        def quantise_h(b, r):
+        def quantise_h(b, r, first, last):
             if not graph(b):
                 return
-            if r == 0:
+            if r == 0 and first == 0:
                 held["h_codes", b] = pool2.tile([P, RELS, FEATS], U32, name="h_codes", align_bytes=64)
                 held["h_scales", b] = pool2.tile([P, RELS, FEATS], U8, name="h_scales", align_bytes=64)
+            cols = slice(first * P, last * P)
             nc.vector.quantize_mx(
-                out=held["h_codes", b][:, r, :].bitcast(FP8X4),
-                scales=held["h_scales", b][:, r, :],
-                in_=held["hg", b, r][:].rearrange("p c t -> p (c t)"),
+                out=held["h_codes", b][:, r, cols].bitcast(FP8X4),
+                scales=held["h_scales", b][:, r, cols],
+                in_=held["hg", b, r][:, cols, :].rearrange("p c t -> p (c t)"),
             )
 
         def attend(q):
@@ -339,7 +363,7 @@ def tile_rgat_pa_t_e_kernel(tc, adj, x, dmask, W_words, W_scales, out):
             return b, 2 * k
 
         def on_gpsimd(q):
-            return 1 < q < STEPS - 4
+            return 1 < q < STEPS - 1
 
         def half_graph(half):
             b, side = divmod(half, 2)
@@ -358,6 +382,10 @@ def tile_rgat_pa_t_e_kernel(tc, adj, x, dmask, W_words, W_scales, out):
                 spread_mask(c + 2)
             if k == 1 or k == 2:
                 transpose_x(c + 2, k - 1)
+            if odd:
+                fold(b, first, first + 2, 4)
+            else:
+                fold(b, first, first + 2, 2)
             reciprocal(s - 1)
             relu_first(s - 4)
             copy_h(hb, piece, nc.scalar.copy)
@@ -368,30 +396,35 @@ def tile_rgat_pa_t_e_kernel(tc, adj, x, dmask, W_words, W_scales, out):
             nb, next_piece = h_pieces(s + 1)
             project(nb, next_piece)
             project(nb, next_piece + 1)
-            if odd:
-                fold(b, first, first + 2, 4)
             if on_gpsimd(s - 1):
                 normalise(s - 1, nc.gpsimd)
             add_mask(b2, first2 + odd, first2 + odd + 1)
             if odd:
                 reduce_max(b, first, first + 2, FOLDS)
-            copy_att(s - 2, nc.vector.tensor_copy)
+            if s >= STEPS - 1:
+                copy_att(s - 2, nc.scalar.copy)
+            else:
+                copy_att(s - 2, nc.vector.tensor_copy)
             if s > 0:
                 exponentials(s, 1)
             add_relus(s - 4)
             if not odd:
-                fold(b, first, first + 2, 2)
+                fold(b, first, first + 2, 3)
             else:
                 fold(b2, first2, first2 + 2, 1)
             copy_h(hb, piece + 1, nc.scalar.copy)
-            if k == 1 or k == 2:
-                quantise_h(c, k - 1)
-                copy_x(c + 2, k - 1, nc.scalar.copy)
             if k == 0:
-                quantise_x(c + 1)
-            if not odd:
-                fold(b, first, first + 2, 3)
+                quantise_h(c, 0, 0, 2)
+            if k == 1:
+                quantise_h(c, 0, 2, 4)
+            if k == 2:
+                quantise_h(c, 1, 0, 4)
+            if k == 3:
+                quantise_x(c + 2)
+            if k == 1 or k == 2:
+                copy_x(c + 2, k - 1, nc.scalar.copy)
 
+        keep_warm(5)
         spread_mask(0)
         for half in range(2):
             transpose_x(0, half)
@@ -412,6 +445,7 @@ def tile_rgat_pa_t_e_kernel(tc, adj, x, dmask, W_words, W_scales, out):
         exponentials(0, 0)
         exponentials(0, 1)
         add_mask(0, 2, 4)
+        quantise_x(1)
         fold(0, 2, 4, 1)
         for piece in range(4):
             copy_h(0, piece, nc.scalar.copy)
@@ -420,15 +454,15 @@ def tile_rgat_pa_t_e_kernel(tc, adj, x, dmask, W_words, W_scales, out):
         for s in range(STEPS):
             step(s)
         last = STEPS - 1
+        transpose_att(last - 1)
         reciprocal(last)
-        for q in (last - 1, last):
-            normalise(q, nc.vector)
-            transpose_att(q)
+        normalise_on_two(last)
+        transpose_att(last)
         quantise_att(last - 2)
         relu_first(last - 3)
         attend(last - 2)
-        add_relus(last - 3)
         copy_att(last - 1, nc.scalar.copy)
+        add_relus(last - 3)
         quantise_att(last - 1)
         attend(last - 1)
         copy_att(last, nc.scalar.copy)

@@ -52,12 +52,12 @@ def tile_rgat_pa_t_e_kernel(tc, adj, x, dmask, W_words, W_scales, out):
         make_identity(nc, ident_bf[:])
         w_codes = consts.tile([P, RELS, FEATS], U32, align_bytes=64)
         w_scales = consts.tile([P, RELS, FEATS], U8, align_bytes=64)
-        mask_rows = consts.tile([P, NODES], BF16)
-        nc.vector.memset(mask_rows[:], 0.0)
-        nc.vector.memset(w_scales[:].bitcast(I32), 0)
+        mask_rows = consts.tile([GRAPHS, NODES], BF16)
         neg_rows = consts.tile([P, NODES], BF16)
+        nc.vector.memset(neg_rows[:], 0.0)
         warm_rows = consts.tile([P, NODES], BF16)
         nc.vector.memset(warm_rows[:], 0.0)
+        nc.vector.memset(w_scales[:].bitcast(I32), 0)
 
         def load_x(b):
             x_sb = loads.tile([P, PACK, FEATS], BF16, name="x_sb")
@@ -86,7 +86,7 @@ def tile_rgat_pa_t_e_kernel(tc, adj, x, dmask, W_words, W_scales, out):
                 in_=adj[b].rearrange("(p j) m r -> p j (m r)", j=TILES)[:, first:last, :],
             )
 
-        nc.sync.dma_start(out=mask_rows[0:GRAPHS, :], in_=dmask.rearrange("b o m -> (b o) m"))
+        nc.sync.dma_start(out=mask_rows[:], in_=dmask.rearrange("b o m -> (b o) m"))
         load_adj(0, 0, 2)
         load_x(0)
         load_x(1)
@@ -97,7 +97,7 @@ def tile_rgat_pa_t_e_kernel(tc, adj, x, dmask, W_words, W_scales, out):
             load_adj(b, 0, 4)
             load_x(b)
 
-        nc.vector.tensor_scalar(out=neg_rows[:], in0=mask_rows[:], scalar1=BIG, scalar2=-BIG, op0=ALU.mult, op1=ALU.add)
+        nc.vector.tensor_scalar(out=neg_rows[0:GRAPHS, :], in0=mask_rows[:], scalar1=BIG, scalar2=-BIG, op0=ALU.mult, op1=ALU.add)
 
         def keep_warm(count):
             for i in range(count):
@@ -180,34 +180,18 @@ def tile_rgat_pa_t_e_kernel(tc, adj, x, dmask, W_words, W_scales, out):
             held["recip", q] = pool3.tile([P, RELS], F32, name="recip")
             nc.vector.reciprocal(out=held["recip", q][:], in_=held["sums", q][:])
 
-        def normalise(q, engine):
+        def normalise(q, r, engine):
             if not row_tile(q):
                 return
-            held["att", q] = pool3.tile([P, RELS, NODES], BF16, name="att")
-            for r in range(RELS):
-                engine.tensor_scalar(
-                    out=held["att", q][:, r, :],
-                    in0=held["e", q][:, r, :],
-                    scalar1=held["recip", q][:, r : r + 1],
-                    scalar2=1.0,
-                    op0=ALU.mult,
-                    op1=ALU.mult,
-                )
-
-        def normalise_on_two(q):
-            held["att", q] = pool3.tile([P, RELS, NODES], BF16, name="att")
-            nc.vector.tensor_scalar(
-                out=held["att", q][:, 0, :],
-                in0=held["e", q][:, 0, :],
-                scalar1=held["recip", q][:, 0:1],
-                scalar2=None,
+            if ("att", q) not in held:
+                held["att", q] = pool3.tile([P, RELS, NODES], BF16, name="att")
+            engine.tensor_scalar(
+                out=held["att", q][:, r, :],
+                in0=held["e", q][:, r, :],
+                scalar1=held["recip", q][:, r : r + 1],
+                scalar2=1.0,
                 op0=ALU.mult,
-            )
-            nc.scalar.activation(
-                out=held["att", q][:, 1, :],
-                in_=held["e", q][:, 1, :],
-                func=FUNC.Copy,
-                scale=held["recip", q][:, 1:2],
+                op1=ALU.mult,
             )
 
         def transpose_att(q):
@@ -362,7 +346,7 @@ def tile_rgat_pa_t_e_kernel(tc, adj, x, dmask, W_words, W_scales, out):
             b, k = divmod(s + 2, TILES)
             return b, 2 * k
 
-        def on_gpsimd(q):
+        def on_gpsimd(q, r):
             return 1 < q < STEPS - 1
 
         def half_graph(half):
@@ -389,24 +373,26 @@ def tile_rgat_pa_t_e_kernel(tc, adj, x, dmask, W_words, W_scales, out):
             reciprocal(s - 1)
             relu_first(s - 4)
             copy_h(hb, piece, nc.scalar.copy)
-            if not on_gpsimd(s - 1):
-                normalise(s - 1, nc.vector)
+            for r in range(RELS):
+                if not on_gpsimd(s - 1, r):
+                    normalise(s - 1, r, nc.vector)
             quantise_att(s - 3)
             attend(s - 3)
             nb, next_piece = h_pieces(s + 1)
             project(nb, next_piece)
             project(nb, next_piece + 1)
-            if on_gpsimd(s - 1):
-                normalise(s - 1, nc.gpsimd)
+            for r in range(RELS):
+                if on_gpsimd(s - 1, r):
+                    normalise(s - 1, r, nc.gpsimd)
             add_mask(b2, first2 + odd, first2 + odd + 1)
             if odd:
                 reduce_max(b, first, first + 2, FOLDS)
+            if s > 0:
+                exponentials(s, 1)
             if s >= STEPS - 1:
                 copy_att(s - 2, nc.scalar.copy)
             else:
                 copy_att(s - 2, nc.vector.tensor_copy)
-            if s > 0:
-                exponentials(s, 1)
             add_relus(s - 4)
             if not odd:
                 fold(b, first, first + 2, 3)
@@ -424,7 +410,7 @@ def tile_rgat_pa_t_e_kernel(tc, adj, x, dmask, W_words, W_scales, out):
             if k == 1 or k == 2:
                 copy_x(c + 2, k - 1, nc.scalar.copy)
 
-        keep_warm(5)
+        keep_warm(2)
         spread_mask(0)
         for half in range(2):
             transpose_x(0, half)
@@ -456,7 +442,8 @@ def tile_rgat_pa_t_e_kernel(tc, adj, x, dmask, W_words, W_scales, out):
         last = STEPS - 1
         transpose_att(last - 1)
         reciprocal(last)
-        normalise_on_two(last)
+        normalise(last, 0, nc.vector)
+        normalise(last, 1, nc.vector)
         transpose_att(last)
         quantise_att(last - 2)
         relu_first(last - 3)

@@ -194,6 +194,18 @@ def tile_rgat_pa_t_e_kernel(tc, adj, x, dmask, W_words, W_scales, out):
                 op1=ALU.mult,
             )
 
+        def normalise_on_scalar(q, r):
+            if not row_tile(q):
+                return
+            if ("att", q) not in held:
+                held["att", q] = pool3.tile([P, RELS, NODES], BF16, name="att")
+            nc.scalar.activation(
+                out=held["att", q][:, r, :],
+                in_=held["e", q][:, r, :],
+                func=FUNC.Copy,
+                scale=held["recip", q][:, r : r + 1],
+            )
+
         def transpose_att(q):
             if not row_tile(q):
                 return
@@ -346,8 +358,11 @@ def tile_rgat_pa_t_e_kernel(tc, adj, x, dmask, W_words, W_scales, out):
             b, k = divmod(s + 2, TILES)
             return b, 2 * k
 
+        def on_scalar(q, r):
+            return r == 1 and q == STEPS - 2
+
         def on_gpsimd(q, r):
-            return 1 < q < STEPS - 1
+            return 1 < q < STEPS - 1 and not on_scalar(q, r)
 
         def half_graph(half):
             b, side = divmod(half, 2)
@@ -374,7 +389,7 @@ def tile_rgat_pa_t_e_kernel(tc, adj, x, dmask, W_words, W_scales, out):
             relu_first(s - 4)
             copy_h(hb, piece, nc.scalar.copy)
             for r in range(RELS):
-                if not on_gpsimd(s - 1, r):
+                if not on_gpsimd(s - 1, r) and not on_scalar(s - 1, r):
                     normalise(s - 1, r, nc.vector)
             quantise_att(s - 3)
             attend(s - 3)
@@ -389,6 +404,9 @@ def tile_rgat_pa_t_e_kernel(tc, adj, x, dmask, W_words, W_scales, out):
                 reduce_max(b, first, first + 2, FOLDS)
             if s > 0:
                 exponentials(s, 1)
+            for r in range(RELS):
+                if on_scalar(s - 1, r):
+                    normalise_on_scalar(s - 1, r)
             if s >= STEPS - 1:
                 copy_att(s - 2, nc.scalar.copy)
             else:

@@ -316,6 +316,10 @@ def tile_rgat_pa_t_e_kernel(tc, adj, x, dmask, W_words, W_scales, out):
             b = q // TILES
             for r in range(RELS):
                 g_r = psum.tile([P, FEATS], F32, name="g_r", tag="bank")
+                if r == 0:
+                    nc.tensor.matmul(
+                        out=g_r[:, 0:256], lhsT=warm_rows[:, 0:P], rhs=warm_rows[:, 0:256], start=True, stop=True
+                    )
                 nc.tensor.matmul_mx(
                     out=g_r[:],
                     lhsT=held["att_codes", q][:, r, :].bitcast(FP8X4),

from contextlib import ExitStack

import concourse.mybir as mybir
from concourse.masks import make_identity

F32 = mybir.dt.float32
BF16 = mybir.dt.bfloat16
I32 = mybir.dt.int32
U32 = mybir.dt.uint32
U8 = mybir.dt.uint8
FP8X4 = mybir.dt.float8_e4m3fn_x4
ALU = mybir.AluOpType
FUNC = mybir.ActivationFunctionType
AXIS = mybir.AxisListType

GRAPHS = 8
NODES = 512
FEATS = 512
RELS = 2
P = 128
PACK = 4
TILES = NODES // P
STEPS = GRAPHS * TILES
BIG = 1.0e30
FOLDS = 4

FLOPS = 2 * GRAPHS * RELS * NODES * FEATS * FEATS + 2 * GRAPHS * RELS * NODES * NODES * FEATS


def tile_rgat_pa_t_e_kernel(tc, adj, x, dmask, W_words, W_scales, out):
    nc = tc.nc
    with ExitStack() as stack:
        consts = stack.enter_context(tc.tile_pool(name="consts", bufs=1))
        loads = stack.enter_context(tc.tile_pool(name="loads", bufs=GRAPHS))
        pool2 = stack.enter_context(tc.tile_pool(name="pool2", bufs=2))
        pool4 = stack.enter_context(tc.tile_pool(name="pool4", bufs=4))
        pool3 = stack.enter_context(tc.tile_pool(name="pool3", bufs=3))
        psum = stack.enter_context(tc.psum_pool(name="psum", bufs=4))
        stack.enter_context(tc.manual_schedule())

        held = {}

        def graph(b):
            return 0 <= b < GRAPHS

        def row_tile(q):
            return 0 <= q < STEPS

        ident = consts.tile([P, P], F32)
        make_identity(nc, ident[:])
        ident_bf = consts.tile([P, P], BF16)
        make_identity(nc, ident_bf[:])
        w_codes = consts.tile([P, RELS, FEATS], U32, align_bytes=64)
        w_scales = consts.tile([P, RELS, FEATS], U8, align_bytes=64)
        mask_rows = consts.tile([GRAPHS, NODES], BF16)
        neg_rows = consts.tile([P, NODES], BF16)
        nc.vector.memset(neg_rows[:], 0.0)
        warm_rows = consts.tile([P, NODES], BF16)
        nc.vector.memset(warm_rows[:], 0.0)
        nc.vector.memset(w_scales[:].bitcast(I32), 0)

        def load_x(b):
            x_sb = loads.tile([P, PACK, FEATS], BF16, name="x_sb")
            nc.sync.dma_start(
                out=x_sb[:].rearrange("p (u e) k -> p u e k", u=2),
                in_=x[b].rearrange("(u p e) k -> p u e k", u=2, e=2),
            )
            held["x_sb", b] = x_sb

        def load_weight():
            for quad in range(4):
                nc.sync.dma_start(
                    out=w_scales[32 * quad : 32 * quad + 4, :, :].bitcast(I32),
                    in_=W_scales[:, 4 * quad : 4 * quad + 4, :].rearrange("g q n -> q g n").bitcast(I32),
                )
            nc.sync.dma_start(
                out=w_codes[:].bitcast(I32),
                in_=W_words.rearrange("g p n t -> p g (n t)").bitcast(I32),
            )

        def load_adj(b, first, last):
            if first == 0:
                held["adj", b] = loads.tile([P, TILES, NODES * RELS], BF16, name="adj_sb")
            nc.sync.dma_start(
                out=held["adj", b][:, first:last, :],
                in_=adj[b].rearrange("(p j) m r -> p j (m r)", j=TILES)[:, first:last, :],
            )

        nc.sync.dma_start(out=mask_rows[:], in_=dmask.rearrange("b o m -> (b o) m"))
        load_adj(0, 0, 2)
        load_x(0)
        load_x(1)
        load_weight()
        load_adj(0, 2, 4)
        load_adj(1, 0, 4)
        for b in range(2, GRAPHS):
            load_adj(b, 0, 4)
            load_x(b)

        nc.vector.tensor_scalar(out=neg_rows[0:GRAPHS, :], in0=mask_rows[:], scalar1=BIG, scalar2=-BIG, op0=ALU.mult, op1=ALU.add)

        def keep_warm(count):
            for i in range(count):
                idle = psum.tile([P, NODES], F32, name="idle", tag="bank")
                nc.tensor.matmul(out=idle[:], lhsT=warm_rows[:, 0:P], rhs=warm_rows[:], start=True, stop=True)

        def spread_mask(b):
            if not graph(b):
                return
            neg = psum.tile([P, NODES, RELS], BF16, name="neg", bufs=2)
            for half in range(2):
                keys = slice(half * NODES // 2, (half + 1) * NODES // 2)
                nc.tensor.matmul(
                    out=neg[:, keys, :],
                    lhsT=ident_bf[:, b : b + 1].to_broadcast([P, P]),
                    rhs=neg_rows[:, keys].unsqueeze(2).to_broadcast([P, NODES // 2, RELS]),
                    start=True,
                    stop=True,
                )
            held["neg", b] = neg

        def add_mask(b, first, last):
            if not graph(b):
                return
            rows = held["adj", b][:, first:last, :]
            nc.vector.tensor_tensor(
                out=rows,
                in0=rows,
                in1=held["neg", b][:].rearrange("p m r -> p (m r)").unsqueeze(1).to_broadcast([P, last - first, NODES * RELS]),
                op=ALU.add,
            )
            if ("negmax", b) not in held:
                held["negmax", b] = pool3.tile([P, TILES, RELS], F32, name="negmax")

        def fold(b, first, last, level):
            if not graph(b):
                return
            width = (NODES * RELS) >> level
            before = held["adj", b] if level == 1 else held["fold", level - 1, b]
            if ("fold", level, b) not in held:
                held["fold", level, b] = pool2.tile([P, TILES, width], BF16, name="fold%d" % level)
            rows = slice(first, last)
            nc.vector.tensor_tensor(
                out=held["fold", level, b][:, rows, :],
                in0=before[:, rows, 0:width],
                in1=before[:, rows, width : 2 * width],
                op=ALU.max,
            )

        def reduce_max(b, first, last, level):
            if not graph(b):
                return
            nc.vector.tensor_reduce(
                out=held["negmax", b][:, first:last, :],
                in_=held["fold", level, b][:, first:last, :].rearrange("p j (m r) -> p j r m", r=RELS),
                axis=AXIS.X,
                op=ALU.max,
                negate=True,
            )

        def exponentials(q, r):
            if not row_tile(q):
                return
            b, j = divmod(q, TILES)
            if r == 0:
                held["e", q] = pool4.tile([P, RELS, NODES], F32, name="e")
                held["sums", q] = pool3.tile([P, RELS], F32, name="sums")
            nc.scalar.activation(
                out=held["e", q][:, r, :],
                in_=held["adj", b][:, j, :].rearrange("p (m r) -> p r m", r=RELS)[:, r, :],
                func=FUNC.Exp,
                bias=held["negmax", b][:, j, r : r + 1],
                scale=1.0,
                accum_out=held["sums", q][:, r : r + 1],
            )

        def reciprocal(q):
            if not row_tile(q):
                return
            held["recip", q] = pool3.tile([P, RELS], F32, name="recip")
            nc.vector.reciprocal(out=held["recip", q][:], in_=held["sums", q][:])

        def normalise(q, r, engine):
            if not row_tile(q):
                return
            if ("att", q) not in held:
                held["att", q] = pool3.tile([P, RELS, NODES], BF16, name="att")
            engine.tensor_scalar(
                out=held["att", q][:, r, :],
                in0=held["e", q][:, r, :],
                scalar1=held["recip", q][:, r : r + 1],
                scalar2=1.0,
                op0=ALU.mult,
                op1=ALU.mult,
            )

        def normalise_on_scalar(q, r):
            if not row_tile(q):
                return
            if ("att", q) not in held:
                held["att", q] = pool3.tile([P, RELS, NODES], BF16, name="att")
            nc.scalar.activation(
                out=held["att", q][:, r, :],
                in_=held["e", q][:, r, :],
                func=FUNC.Copy,
                scale=held["recip", q][:, r : r + 1],
            )

        def transpose_att(q):
            if not row_tile(q):
                return
            aT = psum.tile([P, RELS, 2, P], F32, name="aT", tag="bank")
            for r in range(RELS):
                words = held["att", q][:, r, :].bitcast(F32)
                for u in range(2):
                    nc.tensor.transpose(aT[:, r, u, :], words[:, u * P : (u + 1) * P], ident[:])
            held["aT", q] = aT

        def copy_att(q, copy_out):
            if not row_tile(q):
                return
            held["attg", q] = pool3.tile([P, RELS, P, PACK], BF16, name="attg", align_bytes=64)
            copy_out(
                out=held["attg", q][:].bitcast(F32),
                in_=held["aT", q][:].rearrange("p r u n -> p r n u"),
            )

        def quantise_att(q):
            if not row_tile(q):
                return
            held["att_codes", q] = pool3.tile([P, RELS, P], U32, name="att_codes", align_bytes=64)
            held["att_scales", q] = pool3.tile([P, RELS, P], U8, name="att_scales", align_bytes=64)
            nc.vector.quantize_mx(
                out=held["att_codes", q][:].rearrange("p r n -> p (r n)").bitcast(FP8X4),
                scales=held["att_scales", q][:].rearrange("p r n -> p (r n)"),
                in_=held["attg", q][:].rearrange("p r n t -> p (r n t)"),
            )

        def transpose_x(b, half):
            if not graph(b):
                return
            xT = psum.tile([P, 2, 2, P], F32, name="xT", tag="bank")
            for tt in range(2):
                words = held["x_sb", b][:, 2 * half + tt, :].bitcast(F32)
                for v in range(2):
                    nc.tensor.transpose(xT[:, tt, v, :], words[:, v : FEATS // 2 : 2], ident[:])
            held["xT", b, half] = xT

        def copy_x(b, half, copy_out):
            if not graph(b):
                return
            if half == 0:
                held["xg", b] = pool2.tile([P, PACK, P, PACK], BF16, name="xg", align_bytes=64)
            copy_out(
                out=held["xg", b][:, 2 * half : 2 * half + 2, :, :].bitcast(F32),
                in_=held["xT", b, half][:].rearrange("p tt v n -> p tt n v"),
            )

        def quantise_x(b):
            if not graph(b):
                return
            held["x_codes", b] = pool3.tile([P, NODES], U32, name="x_codes", align_bytes=64)
            held["x_scales", b] = pool3.tile([P, NODES], U8, name="x_scales", align_bytes=64)
            nc.vector.quantize_mx(
                out=held["x_codes", b][:].bitcast(FP8X4),
                scales=held["x_scales", b][:],
                in_=held["xg", b][:].rearrange("p t n k -> p (t n k)"),
            )

        def project(b, piece):
            if not graph(b):
                return
            r, c = divmod(piece, PACK)
            cols = slice(c * P, (c + 1) * P)
            hps = psum.tile([P, PACK, P], F32, name="hps", bufs=2)
            for t in range(PACK):
                rows = slice(t * P, (t + 1) * P)
                nc.tensor.matmul_mx(
                    out=hps[:, t, :],
                    lhsT=held["x_codes", b][:, rows].bitcast(FP8X4),
                    lhsT_scale=held["x_scales", b][:, rows],
                    rhs=w_codes[:, r, cols].bitcast(FP8X4),
                    rhs_scale=w_scales[:, r, cols],
                    start=True,
                    stop=True,
                )
            held["hps", b, piece] = hps

        def copy_h(b, piece, copy_out):
            if not graph(b):
                return
            r, c = divmod(piece, PACK)
            if c == 0:
                held["hg", b, r] = pool3.tile([P, FEATS, PACK], BF16, name="hg", align_bytes=64)
            copy_out(
                out=held["hg", b, r][:, c * P : (c + 1) * P, :],
                in_=held["hps", b, piece][:].rearrange("p t c -> p c t"),
            )

        def quantise_h(b, r, first, last):
            if not graph(b):
                return
            if r == 0 and first == 0:
                held["h_codes", b] = pool2.tile([P, RELS, FEATS], U32, name="h_codes", align_bytes=64)
                held["h_scales", b] = pool2.tile([P, RELS, FEATS], U8, name="h_scales", align_bytes=64)
            cols = slice(first * P, last * P)
            nc.vector.quantize_mx(
                out=held["h_codes", b][:, r, cols].bitcast(FP8X4),
                scales=held["h_scales", b][:, r, cols],
                in_=held["hg", b, r][:, cols, :].rearrange("p c t -> p (c t)"),
            )

        def attend(q):
            if not row_tile(q):
                return
            b = q // TILES
            for r in range(RELS):
                g_r = psum.tile([P, FEATS], F32, name="g_r", tag="bank")
                if r == 0:
                    nc.tensor.matmul(
                        out=g_r[:, 0:256], lhsT=warm_rows[:, 0:P], rhs=warm_rows[:, 0:256], start=True, stop=True
                    )
                nc.tensor.matmul_mx(
                    out=g_r[:],
                    lhsT=held["att_codes", q][:, r, :].bitcast(FP8X4),
                    lhsT_scale=held["att_scales", q][:, r, :],
                    rhs=held["h_codes", b][:, r, :].bitcast(FP8X4),
                    rhs_scale=held["h_scales", b][:, r, :],
                    start=True,
                    stop=True,
                )
                held["g", q, r] = g_r

        def relu_first(q):
            if not row_tile(q):
                return
            held["relu0", q] = pool3.tile([P, FEATS], F32, name="relu0")
            nc.scalar.activation(out=held["relu0", q][:], in_=held["g", q, 0][:], func=FUNC.Relu)

        def add_relus(q):
            if not row_tile(q):
                return
            b, j = divmod(q, TILES)
            if j % 2 == 0:
                held["out_sb", q // 2] = pool2.tile([P, 2, FEATS], F32, name="out_sb")
            out_sb = held["out_sb", q // 2]
            nc.vector.scalar_tensor_tensor(
                out=out_sb[:, j % 2, :],
                in0=held["g", q, 1][:],
                scalar=0.0,
                in1=held["relu0", q][:],
                op0=ALU.max,
                op1=ALU.add,
            )
            out_rows = out[b].rearrange("(p j) h -> p j h", j=TILES)
            if b == GRAPHS - 1:
                nc.sync.dma_start(out=out_rows[:, j, :], in_=out_sb[:, j % 2, :])
            elif j % 2 == 1:
                nc.sync.dma_start(out=out_rows[:, j - 1 : j + 1, :], in_=out_sb[:])

        def h_pieces(s):
            b, k = divmod(s + 2, TILES)
            return b, 2 * k

        def on_scalar(q, r):
            return r == 1 and q == STEPS - 2

        def on_gpsimd(q, r):
            return 1 < q < STEPS - 1 and not on_scalar(q, r)

        def half_graph(half):
            b, side = divmod(half, 2)
            return b, 2 * side

        def step(s):
            c, k = divmod(s, TILES)
            i, odd = divmod(s, 2)
            hb, piece = h_pieces(s)
            b, first = half_graph(i + 1)
            b2, first2 = half_graph(i + 2)
            if s > 0:
                exponentials(s, 0)
            transpose_att(s - 2)
            if k == 3:
                spread_mask(c + 2)
            if k == 1 or k == 2:
                transpose_x(c + 2, k - 1)
            if odd:
                fold(b, first, first + 2, 4)
            else:
                fold(b, first, first + 2, 2)
            reciprocal(s - 1)
            relu_first(s - 4)
            copy_h(hb, piece, nc.scalar.copy)
            for r in range(RELS):
                if not on_gpsimd(s - 1, r) and not on_scalar(s - 1, r):
                    normalise(s - 1, r, nc.vector)
            quantise_att(s - 3)
            attend(s - 3)
            nb, next_piece = h_pieces(s + 1)
            project(nb, next_piece)
            project(nb, next_piece + 1)
            for r in range(RELS):
                if on_gpsimd(s - 1, r):
                    normalise(s - 1, r, nc.gpsimd)
            add_mask(b2, first2 + odd, first2 + odd + 1)
            if odd:
                reduce_max(b, first, first + 2, FOLDS)
            if s > 0:
                exponentials(s, 1)
            for r in range(RELS):
                if on_scalar(s - 1, r):
                    normalise_on_scalar(s - 1, r)
            if s >= STEPS - 1:
                copy_att(s - 2, nc.scalar.copy)
            else:
                copy_att(s - 2, nc.vector.tensor_copy)
            add_relus(s - 4)
            if not odd:
                fold(b, first, first + 2, 3)
            else:
                fold(b2, first2, first2 + 2, 1)
            copy_h(hb, piece + 1, nc.scalar.copy)
            if k == 0:
                quantise_h(c, 0, 0, 2)
            if k == 1:
                quantise_h(c, 0, 2, 4)
            if k == 2:
                quantise_h(c, 1, 0, 4)
            if k == 3:
                quantise_x(c + 2)
            if k == 1 or k == 2:
                copy_x(c + 2, k - 1, nc.scalar.copy)

        keep_warm(2)
        spread_mask(0)
        for half in range(2):
            transpose_x(0, half)
        spread_mask(1)
        for half in range(2):
            transpose_x(1, half)
        add_mask(0, 0, 2)
        for half in range(2):
            copy_x(0, half, nc.scalar.copy)
        for half in range(2):
            copy_x(1, half, nc.scalar.copy)
        fold(0, 0, 2, 1)
        fold(0, 0, 2, 2)
        reduce_max(0, 0, 2, 2)
        quantise_x(0)
        for piece in range(4):
            project(0, piece)
        exponentials(0, 0)
        exponentials(0, 1)
        add_mask(0, 2, 4)
        quantise_x(1)
        fold(0, 2, 4, 1)
        for piece in range(4):
            copy_h(0, piece, nc.scalar.copy)
        project(0, 4)
        project(0, 5)
        for s in range(STEPS):
            step(s)
        last = STEPS - 1
        transpose_att(last - 1)
        reciprocal(last)
        normalise(last, 0, nc.vector)
        normalise(last, 1, nc.vector)
        transpose_att(last)
        quantise_att(last - 2)
        relu_first(last - 3)
        attend(last - 2)
        copy_att(last - 1, nc.scalar.copy)
        add_relus(last - 3)
        quantise_att(last - 1)
        attend(last - 1)
        copy_att(last, nc.scalar.copy)
        relu_first(last - 2)
        quantise_att(last)
        attend(last)
        add_relus(last - 2)
        relu_first(last - 1)
        add_relus(last - 1)
        relu_first(last)
        add_relus(last)
